import numpy as np
import ml_dtypes


def mxq(x, axis, fmt="e4m3"):
    dtype, down = {"e4m3": (ml_dtypes.float8_e4m3fn, 7), "e5m2": (ml_dtypes.float8_e5m2, 14)}[fmt]
    v = np.moveaxis(np.asarray(x, np.float32).astype(ml_dtypes.bfloat16).astype(np.float64), axis, -1)
    blocks = v.reshape(v.shape[:-1] + (-1, 32))
    amax = np.abs(blocks).max(-1, keepdims=True)
    byte = np.maximum(np.where(amax > 0, np.frexp(amax)[1] - 1 + 127, 0) - down, 1)
    scale = np.exp2(byte - 127.0)
    codes = (blocks / scale).astype(np.float32).astype(dtype).astype(np.float64)
    return np.moveaxis((codes * scale).reshape(v.shape), -1, axis)


WIDE = False


def mx_kscale(k):
    if not WIDE:
        return np.ones(k)
    levels = np.array([10, -10, 5, -5, 0])
    a = np.random.permutation(np.resize(levels, k // 512 * 4)).reshape(k // 512, 4)
    idx = np.arange(k)
    return np.exp2(a[idx // 512, idx % 128 // 32])


BF16 = ml_dtypes.bfloat16


def bf(x):
    return np.asarray(x, np.float32).astype(BF16)


def f64(x):
    return np.asarray(x).astype(np.float64)


B, S, D, H, KD, DFF, WIN = 1, 1536, 256, 8, 256, 1024, 128
NEG = 1e9
QB = 2 * WIN
KW = QB + 2 * WIN


def setup_inputs():
    lev = mx_kscale(S)
    hi, lo = lev.max(), lev.min()
    t = np.where(np.arange(S) % WIN < WIN // 2, hi, lo)
    q = np.random.standard_normal((B, S, H, KD)) * 1.2
    k = np.random.standard_normal((B, S, H, KD)) * 1.2
    v = np.random.standard_normal((B, S, H, KD)) * 1.5
    q[..., 0] = np.sqrt(KD)
    k[..., 0] += np.log(t)[None, :, None]
    v = v * (hi / t)[None, :, None, None]
    return {"q": bf(q), "k": bf(k), "v": bf(v)}


def reference(q, k, v):
    qh = f64(q).transpose(0, 2, 1, 3)
    kh = f64(k).transpose(0, 2, 1, 3)
    vq = mxq(f64(v).transpose(0, 2, 1, 3), 2, "e4m3")
    idx = np.arange(S)
    blocks = []
    for i0 in range(0, S, QB):
        k0 = min(max(i0 - WIN, 0), S - KW)
        s = qh[:, :, i0:i0 + QB] @ kh[:, :, k0:k0 + KW].transpose(0, 1, 3, 2) / np.sqrt(KD)
        mask = np.abs(idx[i0:i0 + QB, None] - idx[None, k0:k0 + KW]) <= WIN
        s = s + (1.0 - mask) * (-NEG)
        e = np.exp(s - s.max(-1, keepdims=True))
        blocks.append((mxq(e, 3, "e4m3") @ vq[:, :, k0:k0 + KW]) / e.sum(-1, keepdims=True))
    return np.concatenate(blocks, axis=2).transpose(0, 2, 1, 3)

@@ -1,0 +1,287 @@
+from contextlib import ExitStack
+
+import concourse.mybir as mybir
+from concourse.masks import make_identity
+
+F32 = mybir.dt.float32
+BF16 = mybir.dt.bfloat16
+U32 = mybir.dt.uint32
+U8 = mybir.dt.uint8
+FP8X4 = mybir.dt.float8_e4m3fn_x4
+ALU = mybir.AluOpType
+ACT = mybir.ActivationFunctionType
+AXIS = mybir.AxisListType
+
+P = 128
+SEQ = 1536
+HEADS = 8
+FEAT = 256
+ROW = HEADS * FEAT
+TILES = SEQ // P
+PACK = 4
+K_PASS = P * PACK
+SPAN = 3 * P
+PAIR = 2
+STEPS_PER_TILE = HEADS // PAIR
+STEPS = TILES * STEPS_PER_TILE
+GROUPS = 5
+SCALE = 1.0 / 16.0
+MASKED = -1.0e9 / SCALE
+
+FLOPS = 2 * 2 * HEADS * (SEQ // 256) * 256 * 512 * FEAT
+
+
+def clamp(x, low, high):
+    return max(low, min(x, high))
+
+
+def tile_encoderlayer_pa_kernel(tc, q, k, v, out):
+    nc = tc.nc
+    q_rows = q.rearrange("b s h f -> (b s) (h f)")
+    k_rows = k.rearrange("b s h f -> (b s) (h f)")
+    v_rows = v.rearrange("b s h f -> (b s) (h f)")
+    out_rows = out.rearrange("b s h f -> (b s) (h f)")
+
+    with ExitStack() as stack:
+        const = stack.enter_context(tc.tile_pool(name="const", bufs=1))
+        loads = stack.enter_context(tc.tile_pool(name="loads", bufs=2))
+        work = stack.enter_context(tc.tile_pool(name="work", bufs=3))
+        stats = stack.enter_context(tc.tile_pool(name="stats", bufs=6))
+        psum = stack.enter_context(tc.psum_pool(name="psum", bufs=1))
+
+        ident_f32 = const.tile([P, P], F32)
+        make_identity(nc, ident_f32[:])
+        ident_bf = const.tile([P, P], BF16)
+        make_identity(nc, ident_bf[:])
+
+        mask_f32 = const.tile([P, 4, P], F32)
+        nc.gpsimd.memset(mask_f32[:, 0, :], MASKED)
+        nc.gpsimd.memset(mask_f32[:, 1:3, :], 0.0)
+        nc.gpsimd.memset(mask_f32[:, 3, :], MASKED)
+        nc.gpsimd.affine_select(
+            out=mask_f32[:, 1, :], in_=mask_f32[:, 1, :], compare_op=ALU.is_ge, fill=MASKED,
+            base=0, pattern=[[1, P]], channel_multiplier=-1,
+        )
+        nc.gpsimd.affine_select(
+            out=mask_f32[:, 2, :], in_=mask_f32[:, 2, :], compare_op=ALU.is_ge, fill=MASKED,
+            base=0, pattern=[[-1, P]], channel_multiplier=1,
+        )
+        mask_bf = const.tile([P, 4, P], BF16)
+        nc.vector.tensor_copy(out=mask_bf[:], in_=mask_f32[:])
+
+        e_low = const.tile([P, HEADS, K_PASS], BF16)
+        e_high = const.tile([P, HEADS, K_PASS], BF16)
+        e_tiles = [e_low, e_high]
+        nc.vector.memset(e_low[:].rearrange("q h (u c) -> q (h u) c", u=2)[:, :, 192:256], 0.0)
+        nc.vector.memset(e_high[:].rearrange("q h (u c) -> q (h u) c", u=2)[:, :, 0:64], 0.0)
+
+        kT = const.tile([P, HEADS, SEQ * 2], BF16)
+        kT_words = kT[:].bitcast(F32)
+        kT_feat = kT[:].rearrange("p h (s e) -> p h s e", e=2)
+
+        q_sb = {}
+        k_sb = {}
+        v_raw = {}
+        qT = {}
+        v_codes = {}
+        v_scales = {}
+        in_flight = {}
+
+        def load_q(t):
+            q_tile = loads.tile([P, ROW], BF16, tag="q_tile", bufs=3)
+            nc.sync.dma_start(out=q_tile[:], in_=q_rows[t * P : (t + 1) * P, :])
+            q_sb[t] = q_tile
+
+        def load_k(t):
+            k_tile = loads.tile([P, ROW], BF16, tag="k_tile", bufs=4)
+            nc.sync.dma_start(out=k_tile[:], in_=k_rows[t * P : (t + 1) * P, :])
+            k_sb[t] = k_tile
+
+        def load_v(g):
+            v_tile = loads.tile([P, PACK, ROW], BF16, tag="v_tile", bufs=2)
+            first = 2 * g * P
+            nc.sync.dma_start(
+                out=v_tile[:],
+                in_=v_rows[first : first + K_PASS, :].rearrange("(p j) w -> p j w", j=PACK),
+            )
+            v_raw[g] = v_tile
+            codes = work.tile([P, ROW], U32, tag="v_codes", align_bytes=64)
+            scales = work.tile([P, ROW], U8, tag="v_scales", align_bytes=64)
+            v_codes[g] = codes
+            v_scales[g] = scales
+
+        def transpose_four_heads(rows_sb, first_head, dest):
+            words = rows_sb[:].bitcast(F32)
+            turned = psum.tile([P, 4, P], F32, tag="turned", bufs=3)
+            for i in range(4):
+                h = first_head + i
+                nc.tensor.transpose(turned[:, i, :], words[:, h * P : (h + 1) * P], ident_f32[:])
+            nc.scalar.copy(out=dest, in_=turned[:])
+
+        def transpose_q(t, half):
+            if half == 0:
+                qT_tile = work.tile([P, HEADS, P * 2], BF16, tag="qT_tile", bufs=2)
+                qT[t] = qT_tile
+            dest = qT[t][:].bitcast(F32)[:, 4 * half : 4 * half + 4, :]
+            transpose_four_heads(q_sb[t], 4 * half, dest)
+
+        def transpose_k(t, half):
+            dest = kT_words[:, 4 * half : 4 * half + 4, t * P : (t + 1) * P]
+            transpose_four_heads(k_sb[t], 4 * half, dest)
+
+        def quantise_v(g, h):
+            cols = slice(h * FEAT, (h + 1) * FEAT)
+            v_grouped = work.tile([P, FEAT, PACK], BF16, tag="v_grouped", align_bytes=64)
+            nc.vector.tensor_copy(
+                out=v_grouped[:].rearrange("p (c i) j -> p c j i", i=4),
+                in_=v_raw[g][:, :, cols].rearrange("p j (c i) -> p c j i", i=4),
+            )
+            nc.vector.quantize_mx(
+                out=v_codes[g][:, cols].bitcast(FP8X4),
+                scales=v_scales[g][:, cols],
+                in_=v_grouped[:].rearrange("p w j -> p (w j)"),
+            )
+
+        def scores_and_exp(step):
+            t = step // STEPS_PER_TILE
+            first_head = PAIR * (step % STEPS_PER_TILE)
+            first_key_tile = clamp(t - 1, 0, TILES - 3)
+            window = clamp((t - 1) // 2, 0, GROUPS - 1)
+            quarter = first_key_tile - 2 * window
+            if t == 0:
+                masked_tiles, first_mask = slice(1, 3), 2
+            elif t == TILES - 1:
+                masked_tiles, first_mask = slice(0, 2), 0
+            else:
+                masked_tiles, first_mask = slice(0, 3, 2), 1
+            keys = slice(first_key_tile * P, first_key_tile * P + SPAN)
+            qT_feat = qT[t][:].rearrange("p h (r e) -> p h r e", e=2)
+
+            row_max = stats.tile([P, PAIR], F32, tag="row_max")
+            shift = stats.tile([P, PAIR], F32, tag="shift")
+            row_sum = stats.tile([P, PAIR], F32, tag="row_sum")
+            banks = []
+            for i in range(PAIR):
+                h = first_head + i
+                s_ps = psum.tile([P, SPAN], F32, tag="s_ps", bufs=4)
+                for e in range(2):
+                    nc.tensor.matmul(
+                        out=s_ps[:], lhsT=qT_feat[:, h, :, e], rhs=kT_feat[:, h, keys, e],
+                        start=(e == 0), stop=False,
+                    )
+                nc.tensor.matmul(
+                    out=s_ps[:].rearrange("q (b c) -> q b c", c=P)[:, masked_tiles, :],
+                    lhsT=ident_bf[:], rhs=mask_bf[:, first_mask : first_mask + 2, :],
+                    start=False, stop=True,
+                )
+                nc.vector.tensor_reduce(out=row_max[:, i : i + 1], in_=s_ps[:], axis=AXIS.X, op=ALU.max)
+                banks.append(s_ps)
+            nc.vector.tensor_scalar(out=shift[:], in0=row_max[:], scalar1=-SCALE, scalar2=None, op0=ALU.mult)
+            for i in range(PAIR):
+                h = first_head + i
+                e_view = e_tiles[quarter][:, h, :].rearrange("q (u p e) -> q u p e", u=2, e=2)
+                nc.scalar.activation(
+                    out=e_view[:, :, 32 * quarter : 32 * quarter + 96, :],
+                    in_=banks[i][:].rearrange("q (p u e) -> q u p e", u=2, e=2),
+                    func=ACT.Exp, bias=shift[:, i : i + 1], scale=SCALE,
+                    accum_out=row_sum[:, i : i + 1],
+                )
+            in_flight[step] = {
+                "t": t, "first_head": first_head, "window": window, "quarter": quarter,
+                "row_sum": row_sum,
+            }
+
+        def transpose_and_quantise_e(step):
+            state = in_flight[step]
+            e_words = e_tiles[state["quarter"]][:].bitcast(F32)
+            turned = psum.tile([P, PAIR, 2, P], F32, tag="turned", bufs=3)
+            for i in range(PAIR):
+                h = state["first_head"] + i
+                for u in range(2):
+                    nc.tensor.transpose(turned[:, i, u, :], e_words[:, h, u * P : (u + 1) * P], ident_f32[:])
+            e_grouped = work.tile([P, PAIR * P * PACK], BF16, tag="e_grouped", align_bytes=64)
+            nc.vector.tensor_copy(
+                out=e_grouped[:].bitcast(F32).rearrange("p (i q u) -> p i q u", i=PAIR, u=2),
+                in_=turned[:].rearrange("p i u q -> p i q u"),
+            )
+            e_codes = work.tile([P, PAIR * P], U32, tag="e_codes", align_bytes=64)
+            e_scales = work.tile([P, PAIR * P], U8, tag="e_scales", align_bytes=64)
+            nc.vector.quantize_mx(out=e_codes[:].bitcast(FP8X4), scales=e_scales[:], in_=e_grouped[:])
+            state["e_codes"] = e_codes
+            state["e_scales"] = e_scales
+
+        def weighted_sum_and_store(step):
+            state = in_flight[step]
+            t = state["t"]
+            g = state["window"]
+            first_head = state["first_head"]
+            inverse = stats.tile([P, PAIR], F32, tag="inverse")
+            nc.vector.reciprocal(out=inverse[:], in_=state["row_sum"][:])
+            o_ps = psum.tile([P, PAIR, FEAT], F32, tag="o_ps", bufs=1)
+            o_sb = work.tile([P, PAIR, FEAT], F32, tag="o_sb", bufs=4)
+            for i in range(PAIR):
+                h = first_head + i
+                queries = slice(i * P, (i + 1) * P)
+                cols = slice(h * FEAT, (h + 1) * FEAT)
+                nc.tensor.matmul_mx(
+                    out=o_ps[:, i, :],
+                    lhsT=state["e_codes"][:, queries].bitcast(FP8X4),
+                    lhsT_scale=state["e_scales"][:, queries],
+                    rhs=v_codes[g][:, cols].bitcast(FP8X4),
+                    rhs_scale=v_scales[g][:, cols],
+                    start=True, stop=True,
+                )
+            for i in range(PAIR):
+                nc.scalar.activation(
+                    out=o_sb[:, i, :], in_=o_ps[:, i, :], func=ACT.Copy, scale=inverse[:, i : i + 1],
+                )
+            nc.sync.dma_start(
+                out=out_rows[t * P : (t + 1) * P, first_head * FEAT : (first_head + PAIR) * FEAT],
+                in_=o_sb[:].rearrange("q i f -> q (i f)"),
+            )
+
+        def prepare_ahead(step):
+            t = step // STEPS_PER_TILE
+            part = step % STEPS_PER_TILE
+            if part < 2 and t + 1 < TILES:
+                transpose_q(t + 1, part)
+            if part >= 2 and 3 <= t + 2 < TILES:
+                transpose_k(t + 2, part - 2)
+            if t == 0:
+                quantise_v(0, PAIR * part)
+                quantise_v(0, PAIR * part + 1)
+            elif t <= 2 * (GROUPS - 1):
+                quantise_v((t + 1) // 2, ((t + 1) % 2) * STEPS_PER_TILE + part)
+
+        def loads_ahead(t):
+            if t + 2 < TILES:
+                load_q(t + 2)
+            if t + 4 < TILES:
+                load_k(t + 4)
+            if t % 2 == 1 and (t + 3) // 2 < GROUPS:
+                load_v((t + 3) // 2)
+
+        load_q(0)
+        load_k(0)
+        load_k(1)
+        load_k(2)
+        load_v(0)
+        load_q(1)
+        load_k(3)
+        load_v(1)
+        for half in range(2):
+            transpose_q(0, half)
+        for t in range(3):
+            for half in range(2):
+                transpose_k(t, half)
+
+        for step in range(STEPS + 2):
+            if step < STEPS:
+                if step % STEPS_PER_TILE == 0:
+                    loads_ahead(step // STEPS_PER_TILE)
+                scores_and_exp(step)
+                prepare_ahead(step)
+            if 1 <= step <= STEPS:
+                transpose_and_quantise_e(step - 1)
+            if step >= 2:
+                weighted_sum_and_store(step - 2)

@@ -87,111 +87,141 @@ def tile_encoderlayer_pa_kernel(tc, q, k, v, out):
         v_scales = {}
         in_flight = {}
 
-        def load_q(t):
-            q_tile = loads.tile([P, ROW], BF16, tag="q_tile", bufs=3)
-            nc.sync.dma_start(out=q_tile[:], in_=q_rows[t * P : (t + 1) * P, :])
-            q_sb[t] = q_tile
+        def load_rows(rows, t, half, tag, bufs):
+            half_tile = loads.tile([P, ROW // 2], BF16, tag=tag, bufs=bufs, name="half_tile")
+            cols = slice(half * (ROW // 2), (half + 1) * (ROW // 2))
+            nc.sync.dma_start(out=half_tile[:], in_=rows[t * P : (t + 1) * P, cols])
+            return half_tile
 
-        def load_k(t):
-            k_tile = loads.tile([P, ROW], BF16, tag="k_tile", bufs=4)
-            nc.sync.dma_start(out=k_tile[:], in_=k_rows[t * P : (t + 1) * P, :])
-            k_sb[t] = k_tile
+        def load_q(t, half):
+            q_sb[(t, half)] = load_rows(q_rows, t, half, "q_half", 6)
 
-        def load_v(g):
-            v_tile = loads.tile([P, PACK, ROW], BF16, tag="v_tile", bufs=2)
+        def load_k(t, half):
+            k_sb[(t, half)] = load_rows(k_rows, t, half, "k_half", 8)
+
+        def load_v(g, half):
+            if half == 0:
+                v_tile = loads.tile([P, PACK, ROW], BF16, tag="v_tile", bufs=2)
+                codes = work.tile([P, ROW], U32, tag="v_codes", align_bytes=64)
+                scales = work.tile([P, ROW], U8, tag="v_scales", align_bytes=64)
+                v_raw[g] = v_tile
+                v_codes[g] = codes
+                v_scales[g] = scales
             first = 2 * g * P
+            cols = slice(half * (ROW // 2), (half + 1) * (ROW // 2))
             nc.sync.dma_start(
-                out=v_tile[:],
-                in_=v_rows[first : first + K_PASS, :].rearrange("(p j) w -> p j w", j=PACK),
+                out=v_raw[g][:, :, cols],
+                in_=v_rows[first : first + K_PASS, cols].rearrange("(p j) w -> p j w", j=PACK),
             )
-            v_raw[g] = v_tile
-            codes = work.tile([P, ROW], U32, tag="v_codes", align_bytes=64)
-            scales = work.tile([P, ROW], U8, tag="v_scales", align_bytes=64)
-            v_codes[g] = codes
-            v_scales[g] = scales
 
-        def transpose_four_heads(rows_sb, first_head, dest):
-            words = rows_sb[:].bitcast(F32)
+        def copy_out(on_scalar, dest, source):
+            if on_scalar:
+                nc.scalar.copy(out=dest, in_=source)
+            else:
+                nc.vector.tensor_copy(out=dest, in_=source)
+
+        def transpose_four_heads(half_tile, dest, on_scalar):
+            words = half_tile[:].bitcast(F32)
             turned = psum.tile([P, 4, P], F32, tag="turned", bufs=3)
             for i in range(4):
-                h = first_head + i
-                nc.tensor.transpose(turned[:, i, :], words[:, h * P : (h + 1) * P], ident_f32[:])
-            nc.scalar.copy(out=dest, in_=turned[:])
+                nc.tensor.transpose(turned[:, i, :], words[:, i * P : (i + 1) * P], ident_f32[:])
+            copy_out(on_scalar, dest, turned[:])
 
-        def transpose_q(t, half):
+        def transpose_q(t, half, on_scalar):
             if half == 0:
                 qT_tile = work.tile([P, HEADS, P * 2], BF16, tag="qT_tile", bufs=2)
                 qT[t] = qT_tile
             dest = qT[t][:].bitcast(F32)[:, 4 * half : 4 * half + 4, :]
-            transpose_four_heads(q_sb[t], 4 * half, dest)
+            transpose_four_heads(q_sb[(t, half)], dest, on_scalar)
 
-        def transpose_k(t, half):
+        def transpose_k(t, half, on_scalar):
             dest = kT_words[:, 4 * half : 4 * half + 4, t * P : (t + 1) * P]
-            transpose_four_heads(k_sb[t], 4 * half, dest)
+            transpose_four_heads(k_sb[(t, half)], dest, on_scalar)
 
-        def quantise_v(g, h):
+        def regroup_v(g, h):
             cols = slice(h * FEAT, (h + 1) * FEAT)
-            v_grouped = work.tile([P, FEAT, PACK], BF16, tag="v_grouped", align_bytes=64)
+            v_grouped = work.tile([P, FEAT, PACK], BF16, tag="v_grouped", bufs=4, align_bytes=64)
             nc.vector.tensor_copy(
                 out=v_grouped[:].rearrange("p (c i) j -> p c j i", i=4),
                 in_=v_raw[g][:, :, cols].rearrange("p j (c i) -> p c j i", i=4),
             )
+            return v_grouped
+
+        def quantise_v(g, h, v_grouped):
+            cols = slice(h * FEAT, (h + 1) * FEAT)
             nc.vector.quantize_mx(
                 out=v_codes[g][:, cols].bitcast(FP8X4),
                 scales=v_scales[g][:, cols],
                 in_=v_grouped[:].rearrange("p w j -> p (w j)"),
             )
 
-        def scores_and_exp(step):
+        def v_heads_of(step):
             t = step // STEPS_PER_TILE
-            first_head = PAIR * (step % STEPS_PER_TILE)
+            part = step % STEPS_PER_TILE
+            heads = []
+            if 1 <= step <= STEPS_PER_TILE:
+                heads.extend([(0, PAIR * (step - 1)), (0, PAIR * (step - 1) + 1)])
+            if 1 <= t <= 2 * (GROUPS - 1):
+                heads.append(((t + 1) // 2, ((t + 1) % 2) * STEPS_PER_TILE + part))
+            return heads
+
+        def begin(step):
+            t = step // STEPS_PER_TILE
             first_key_tile = clamp(t - 1, 0, TILES - 3)
             window = clamp((t - 1) // 2, 0, GROUPS - 1)
-            quarter = first_key_tile - 2 * window
+            row_max = stats.tile([P, PAIR], F32, tag="row_max")
+            shift = stats.tile([P, PAIR], F32, tag="shift")
+            row_sum = stats.tile([P, PAIR], F32, tag="row_sum")
+            in_flight[step] = {
+                "t": t, "first_head": PAIR * (step % STEPS_PER_TILE),
+                "first_key_tile": first_key_tile, "window": window,
+                "quarter": first_key_tile - 2 * window,
+                "row_max": row_max, "shift": shift, "row_sum": row_sum, "banks": [],
+            }
+
+        def scores(step, i):
+            state = in_flight[step]
+            t = state["t"]
+            h = state["first_head"] + i
             if t == 0:
                 masked_tiles, first_mask = slice(1, 3), 2
             elif t == TILES - 1:
                 masked_tiles, first_mask = slice(0, 2), 0
             else:
                 masked_tiles, first_mask = slice(0, 3, 2), 1
-            keys = slice(first_key_tile * P, first_key_tile * P + SPAN)
+            keys = slice(state["first_key_tile"] * P, state["first_key_tile"] * P + SPAN)
             qT_feat = qT[t][:].rearrange("p h (r e) -> p h r e", e=2)
-
-            row_max = stats.tile([P, PAIR], F32, tag="row_max")
-            shift = stats.tile([P, PAIR], F32, tag="shift")
-            row_sum = stats.tile([P, PAIR], F32, tag="row_sum")
-            banks = []
-            for i in range(PAIR):
-                h = first_head + i
-                s_ps = psum.tile([P, SPAN], F32, tag="s_ps", bufs=4)
-                for e in range(2):
-                    nc.tensor.matmul(
-                        out=s_ps[:], lhsT=qT_feat[:, h, :, e], rhs=kT_feat[:, h, keys, e],
-                        start=(e == 0), stop=False,
-                    )
+            s_ps = psum.tile([P, SPAN], F32, tag="s_ps", bufs=4)
+            for e in range(2):
                 nc.tensor.matmul(
-                    out=s_ps[:].rearrange("q (b c) -> q b c", c=P)[:, masked_tiles, :],
-                    lhsT=ident_bf[:], rhs=mask_bf[:, first_mask : first_mask + 2, :],
-                    start=False, stop=True,
+                    out=s_ps[:], lhsT=qT_feat[:, h, :, e], rhs=kT_feat[:, h, keys, e],
+                    start=(e == 0), stop=False,
                 )
-                nc.vector.tensor_reduce(out=row_max[:, i : i + 1], in_=s_ps[:], axis=AXIS.X, op=ALU.max)
-                banks.append(s_ps)
-            nc.vector.tensor_scalar(out=shift[:], in0=row_max[:], scalar1=-SCALE, scalar2=None, op0=ALU.mult)
+            nc.tensor.matmul(
+                out=s_ps[:].rearrange("q (b c) -> q b c", c=P)[:, masked_tiles, :],
+                lhsT=ident_bf[:], rhs=mask_bf[:, first_mask : first_mask + 2, :],
+                start=False, stop=True,
+            )
+            nc.vector.tensor_reduce(out=state["row_max"][:, i : i + 1], in_=s_ps[:], axis=AXIS.X, op=ALU.max)
+            state["banks"].append(s_ps)
+
+        def exponentials(step):
+            state = in_flight[step]
+            quarter = state["quarter"]
+            nc.vector.tensor_scalar(
+                out=state["shift"][:], in0=state["row_max"][:], scalar1=-SCALE, scalar2=None, op0=ALU.mult,
+            )
             for i in range(PAIR):
-                h = first_head + i
+                h = state["first_head"] + i
                 e_view = e_tiles[quarter][:, h, :].rearrange("q (u p e) -> q u p e", u=2, e=2)
                 nc.scalar.activation(
                     out=e_view[:, :, 32 * quarter : 32 * quarter + 96, :],
-                    in_=banks[i][:].rearrange("q (p u e) -> q u p e", u=2, e=2),
-                    func=ACT.Exp, bias=shift[:, i : i + 1], scale=SCALE,
-                    accum_out=row_sum[:, i : i + 1],
+                    in_=state["banks"][i][:].rearrange("q (p u e) -> q u p e", u=2, e=2),
+                    func=ACT.Exp, bias=state["shift"][:, i : i + 1], scale=SCALE,
+                    accum_out=state["row_sum"][:, i : i + 1],
                 )
-            in_flight[step] = {
-                "t": t, "first_head": first_head, "window": window, "quarter": quarter,
-                "row_sum": row_sum,
-            }
 
-        def transpose_and_quantise_e(step):
+        def transpose_e(step):
             state = in_flight[step]
             e_words = e_tiles[state["quarter"]][:].bitcast(F32)
             turned = psum.tile([P, PAIR, 2, P], F32, tag="turned", bufs=3)
@@ -200,23 +230,34 @@ def tile_encoderlayer_pa_kernel(tc, q, k, v, out):
                 for u in range(2):
                     nc.tensor.transpose(turned[:, i, u, :], e_words[:, h, u * P : (u + 1) * P], ident_f32[:])
             e_grouped = work.tile([P, PAIR * P * PACK], BF16, tag="e_grouped", align_bytes=64)
-            nc.vector.tensor_copy(
-                out=e_grouped[:].bitcast(F32).rearrange("p (i q u) -> p i q u", i=PAIR, u=2),
-                in_=turned[:].rearrange("p i u q -> p i q u"),
+            copy_out(
+                step % 2 == 1,
+                e_grouped[:].bitcast(F32).rearrange("p (i q u) -> p i q u", i=PAIR, u=2),
+                turned[:].rearrange("p i u q -> p i q u"),
             )
+            state["e_grouped"] = e_grouped
+
+        def quantise_e(step):
+            state = in_flight[step]
             e_codes = work.tile([P, PAIR * P], U32, tag="e_codes", align_bytes=64)
             e_scales = work.tile([P, PAIR * P], U8, tag="e_scales", align_bytes=64)
-            nc.vector.quantize_mx(out=e_codes[:].bitcast(FP8X4), scales=e_scales[:], in_=e_grouped[:])
+            nc.vector.quantize_mx(
+                out=e_codes[:].bitcast(FP8X4), scales=e_scales[:], in_=state["e_grouped"][:],
+            )
             state["e_codes"] = e_codes
             state["e_scales"] = e_scales
+
+        def invert_row_sums(step):
+            state = in_flight[step]
+            inverse = stats.tile([P, PAIR], F32, tag="inverse")
+            nc.vector.reciprocal(out=inverse[:], in_=state["row_sum"][:])
+            state["inverse"] = inverse
 
         def weighted_sum_and_store(step):
             state = in_flight[step]
             t = state["t"]
             g = state["window"]
             first_head = state["first_head"]
-            inverse = stats.tile([P, PAIR], F32, tag="inverse")
-            nc.vector.reciprocal(out=inverse[:], in_=state["row_sum"][:])
             o_ps = psum.tile([P, PAIR, FEAT], F32, tag="o_ps", bufs=1)
             o_sb = work.tile([P, PAIR, FEAT], F32, tag="o_sb", bufs=4)
             for i in range(PAIR):
@@ -233,55 +274,69 @@ def tile_encoderlayer_pa_kernel(tc, q, k, v, out):
                 )
             for i in range(PAIR):
                 nc.scalar.activation(
-                    out=o_sb[:, i, :], in_=o_ps[:, i, :], func=ACT.Copy, scale=inverse[:, i : i + 1],
+                    out=o_sb[:, i, :], in_=o_ps[:, i, :], func=ACT.Copy,
+                    scale=state["inverse"][:, i : i + 1],
                 )
             nc.sync.dma_start(
                 out=out_rows[t * P : (t + 1) * P, first_head * FEAT : (first_head + PAIR) * FEAT],
                 in_=o_sb[:].rearrange("q i f -> q (i f)"),
             )
 
-        def prepare_ahead(step):
+        def transposes_ahead(step):
             t = step // STEPS_PER_TILE
             part = step % STEPS_PER_TILE
             if part < 2 and t + 1 < TILES:
-                transpose_q(t + 1, part)
+                transpose_q(t + 1, part, True)
             if part >= 2 and 3 <= t + 2 < TILES:
-                transpose_k(t + 2, part - 2)
-            if t == 0:
-                quantise_v(0, PAIR * part)
-                quantise_v(0, PAIR * part + 1)
-            elif t <= 2 * (GROUPS - 1):
-                quantise_v((t + 1) // 2, ((t + 1) % 2) * STEPS_PER_TILE + part)
+                transpose_k(t + 2, part - 2, True)
 
         def loads_ahead(t):
-            if t + 2 < TILES:
-                load_q(t + 2)
-            if t + 4 < TILES:
-                load_k(t + 4)
-            if t % 2 == 1 and (t + 3) // 2 < GROUPS:
-                load_v((t + 3) // 2)
-
-        load_q(0)
-        load_k(0)
-        load_k(1)
-        load_k(2)
-        load_v(0)
-        load_q(1)
-        load_k(3)
-        load_v(1)
-        for half in range(2):
-            transpose_q(0, half)
-        for t in range(3):
             for half in range(2):
-                transpose_k(t, half)
+                if t + 2 < TILES:
+                    load_q(t + 2, half)
+            for half in range(2):
+                if t + 4 < TILES:
+                    load_k(t + 4, half)
+            for half in range(2):
+                if t % 2 == 1 and (t + 3) // 2 < GROUPS:
+                    load_v((t + 3) // 2, half)
 
-        for step in range(STEPS + 2):
+        stack.enter_context(tc.manual_schedule())
+        for half in range(2):
+            load_q(0, half)
+            for t in range(3):
+                load_k(t, half)
+            load_v(0, half)
+        for half in range(2):
+            load_q(1, half)
+        for half in range(2):
+            load_k(3, half)
+        for half in range(2):
+            load_v(1, half)
+        for half in range(2):
+            transpose_q(0, half, True)
+            for t in range(3):
+                transpose_k(t, half, t % 2 == 1)
+
+        for step in range(STEPS + 3):
+            if 0 <= step - 3:
+                quantise_e(step - 3)
+            if 0 <= step - 2 < STEPS:
+                transpose_e(step - 2)
             if step < STEPS:
                 if step % STEPS_PER_TILE == 0:
                     loads_ahead(step // STEPS_PER_TILE)
-                scores_and_exp(step)
-                prepare_ahead(step)
-            if 1 <= step <= STEPS:
-                transpose_and_quantise_e(step - 1)
-            if step >= 2:
-                weighted_sum_and_store(step - 2)
+                transposes_ahead(step)
+            v_heads = v_heads_of(step)
+            v_grouped_tiles = [regroup_v(g, h) for (g, h) in v_heads]
+            if step < STEPS:
+                begin(step)
+                scores(step, 0)
+            for (g, h), v_grouped_tile in zip(v_heads, v_grouped_tiles):
+                quantise_v(g, h, v_grouped_tile)
+            if 0 <= step - 3:
+                invert_row_sums(step - 3)
+                weighted_sum_and_store(step - 3)
+            if step < STEPS:
+                scores(step, 1)
+                exponentials(step)

@@ -25,6 +25,8 @@ PAIR = 2
 STEPS_PER_TILE = HEADS // PAIR
 STEPS = TILES * STEPS_PER_TILE
 GROUPS = 5
+CHUNKS = GROUPS * HEADS
+V_AHEAD = 4
 SCALE = 1.0 / 16.0
 MASKED = -1.0e9 / SCALE
 
@@ -66,8 +68,17 @@ def tile_encoderlayer_pa_kernel(tc, q, k, v, out):
             out=mask_f32[:, 2, :], in_=mask_f32[:, 2, :], compare_op=ALU.is_ge, fill=MASKED,
             base=0, pattern=[[-1, P]], channel_multiplier=1,
         )
+        key_order = const.tile([P, P], F32)
+        nc.vector.tensor_copy(
+            out=key_order[:].rearrange("i (u c e) -> i u c e", u=2, e=2),
+            in_=ident_f32[:].rearrange("i (c u e) -> i u c e", u=2, e=2),
+        )
         mask_bf = const.tile([P, 4, P], BF16)
-        nc.vector.tensor_copy(out=mask_bf[:], in_=mask_f32[:])
+        for block in range(4):
+            nc.vector.tensor_copy(
+                out=mask_bf[:, block, :].rearrange("q (u c e) -> q u c e", u=2, e=2),
+                in_=mask_f32[:, block, :].rearrange("q (c u e) -> q u c e", u=2, e=2),
+            )
 
         e_low = const.tile([P, HEADS, K_PASS], BF16)
         e_high = const.tile([P, HEADS, K_PASS], BF16)
@@ -86,6 +97,7 @@ def tile_encoderlayer_pa_kernel(tc, q, k, v, out):
         v_codes = {}
         v_scales = {}
         in_flight = {}
+        v_grouped_tiles = {}
 
         def load_rows(rows, t, half, tag, bufs):
             half_tile = loads.tile([P, ROW // 2], BF16, tag=tag, bufs=bufs, name="half_tile")
@@ -99,16 +111,16 @@ def tile_encoderlayer_pa_kernel(tc, q, k, v, out):
         def load_k(t, half):
             k_sb[(t, half)] = load_rows(k_rows, t, half, "k_half", 8)
 
-        def load_v(g, half):
-            if half == 0:
-                v_tile = loads.tile([P, PACK, ROW], BF16, tag="v_tile", bufs=2)
+        def load_v(g, pair):
+            if pair == 0:
+                v_tile = loads.tile([P, PACK, ROW], BF16, tag="v_tile", bufs=3)
                 codes = work.tile([P, ROW], U32, tag="v_codes", align_bytes=64)
                 scales = work.tile([P, ROW], U8, tag="v_scales", align_bytes=64)
                 v_raw[g] = v_tile
                 v_codes[g] = codes
                 v_scales[g] = scales
             first = 2 * g * P
-            cols = slice(half * (ROW // 2), (half + 1) * (ROW // 2))
+            cols = slice(pair * PAIR * FEAT, (pair + 1) * PAIR * FEAT)
             nc.sync.dma_start(
                 out=v_raw[g][:, :, cols],
                 in_=v_rows[first : first + K_PASS, cols].rearrange("(p j) w -> p j w", j=PACK),
@@ -120,11 +132,11 @@ def tile_encoderlayer_pa_kernel(tc, q, k, v, out):
             else:
                 nc.vector.tensor_copy(out=dest, in_=source)
 
-        def transpose_four_heads(half_tile, dest, on_scalar):
+        def transpose_four_heads(half_tile, order, dest, on_scalar):
             words = half_tile[:].bitcast(F32)
             turned = psum.tile([P, 4, P], F32, tag="turned", bufs=3)
             for i in range(4):
-                nc.tensor.transpose(turned[:, i, :], words[:, i * P : (i + 1) * P], ident_f32[:])
+                nc.tensor.transpose(turned[:, i, :], words[:, i * P : (i + 1) * P], order[:])
             copy_out(on_scalar, dest, turned[:])
 
         def transpose_q(t, half, on_scalar):
@@ -132,51 +144,42 @@ def tile_encoderlayer_pa_kernel(tc, q, k, v, out):
                 qT_tile = work.tile([P, HEADS, P * 2], BF16, tag="qT_tile", bufs=2)
                 qT[t] = qT_tile
             dest = qT[t][:].bitcast(F32)[:, 4 * half : 4 * half + 4, :]
-            transpose_four_heads(q_sb[(t, half)], dest, on_scalar)
+            transpose_four_heads(q_sb[(t, half)], ident_f32, dest, on_scalar)
 
         def transpose_k(t, half, on_scalar):
             dest = kT_words[:, 4 * half : 4 * half + 4, t * P : (t + 1) * P]
-            transpose_four_heads(k_sb[(t, half)], dest, on_scalar)
+            transpose_four_heads(k_sb[(t, half)], key_order, dest, on_scalar)
 
-        def regroup_v(g, h):
-            cols = slice(h * FEAT, (h + 1) * FEAT)
-            v_grouped = work.tile([P, FEAT, PACK], BF16, tag="v_grouped", bufs=4, align_bytes=64)
-            nc.vector.tensor_copy(
-                out=v_grouped[:].rearrange("p (c i) j -> p c j i", i=4),
-                in_=v_raw[g][:, :, cols].rearrange("p j (c i) -> p c j i", i=4),
+        def regroup_v(chunk):
+            g, h = chunk // HEADS, chunk % HEADS
+            v_grouped = work.tile([P, FEAT, PACK], BF16, tag="v_grouped", bufs=V_AHEAD, align_bytes=64)
+            nc.gpsimd.tensor_scalar(
+                out=v_grouped[:],
+                in0=v_raw[g][:, :, h * FEAT : (h + 1) * FEAT].rearrange("p j w -> p w j"),
+                scalar1=1.0, scalar2=0.0, op0=ALU.mult, op1=ALU.add,
             )
-            return v_grouped
+            v_grouped_tiles[chunk] = v_grouped
 
-        def quantise_v(g, h, v_grouped):
+        def quantise_v(chunk):
+            g, h = chunk // HEADS, chunk % HEADS
             cols = slice(h * FEAT, (h + 1) * FEAT)
             nc.vector.quantize_mx(
                 out=v_codes[g][:, cols].bitcast(FP8X4),
                 scales=v_scales[g][:, cols],
-                in_=v_grouped[:].rearrange("p w j -> p (w j)"),
+                in_=v_grouped_tiles[chunk][:].rearrange("p w j -> p (w j)"),
             )
-
-        def v_heads_of(step):
-            t = step // STEPS_PER_TILE
-            part = step % STEPS_PER_TILE
-            heads = []
-            if 1 <= step <= STEPS_PER_TILE:
-                heads.extend([(0, PAIR * (step - 1)), (0, PAIR * (step - 1) + 1)])
-            if 1 <= t <= 2 * (GROUPS - 1):
-                heads.append(((t + 1) // 2, ((t + 1) % 2) * STEPS_PER_TILE + part))
-            return heads
 
         def begin(step):
             t = step // STEPS_PER_TILE
             first_key_tile = clamp(t - 1, 0, TILES - 3)
             window = clamp((t - 1) // 2, 0, GROUPS - 1)
-            row_max = stats.tile([P, PAIR], F32, tag="row_max")
             shift = stats.tile([P, PAIR], F32, tag="shift")
             row_sum = stats.tile([P, PAIR], F32, tag="row_sum")
             in_flight[step] = {
                 "t": t, "first_head": PAIR * (step % STEPS_PER_TILE),
                 "first_key_tile": first_key_tile, "window": window,
                 "quarter": first_key_tile - 2 * window,
-                "row_max": row_max, "shift": shift, "row_sum": row_sum, "banks": [],
+                "shift": shift, "row_sum": row_sum, "banks": [],
             }
 
         def scores(step, i):
@@ -202,21 +205,22 @@ def tile_encoderlayer_pa_kernel(tc, q, k, v, out):
                 lhsT=ident_bf[:], rhs=mask_bf[:, first_mask : first_mask + 2, :],
                 start=False, stop=True,
             )
-            nc.vector.tensor_reduce(out=state["row_max"][:, i : i + 1], in_=s_ps[:], axis=AXIS.X, op=ALU.max)
+            unused = work.tile([P, SPAN], F32, tag="unused", bufs=4)
+            nc.vector.tensor_scalar(
+                out=unused[:], in0=s_ps[:], scalar1=-SCALE, scalar2=None, op0=ALU.mult, op1=ALU.min,
+                accum_out=state["shift"][:, i : i + 1],
+            )
             state["banks"].append(s_ps)
 
         def exponentials(step):
             state = in_flight[step]
             quarter = state["quarter"]
-            nc.vector.tensor_scalar(
-                out=state["shift"][:], in0=state["row_max"][:], scalar1=-SCALE, scalar2=None, op0=ALU.mult,
-            )
             for i in range(PAIR):
                 h = state["first_head"] + i
-                e_view = e_tiles[quarter][:, h, :].rearrange("q (u p e) -> q u p e", u=2, e=2)
+                e_view = e_tiles[quarter][:, h, :].rearrange("q (u b x) -> q b u x", u=2, b=4)
                 nc.scalar.activation(
-                    out=e_view[:, :, 32 * quarter : 32 * quarter + 96, :],
-                    in_=state["banks"][i][:].rearrange("q (p u e) -> q u p e", u=2, e=2),
+                    out=e_view[:, quarter : quarter + 3, :, :],
+                    in_=state["banks"][i][:].rearrange("q (b u x) -> q b u x", b=3, u=2),
                     func=ACT.Exp, bias=state["shift"][:, i : i + 1], scale=SCALE,
                     accum_out=state["row_sum"][:, i : i + 1],
                 )
@@ -231,7 +235,7 @@ def tile_encoderlayer_pa_kernel(tc, q, k, v, out):
                     nc.tensor.transpose(turned[:, i, u, :], e_words[:, h, u * P : (u + 1) * P], ident_f32[:])
             e_grouped = work.tile([P, PAIR * P * PACK], BF16, tag="e_grouped", align_bytes=64)
             copy_out(
-                step % 2 == 1,
+                True,
                 e_grouped[:].bitcast(F32).rearrange("p (i q u) -> p i q u", i=PAIR, u=2),
                 turned[:].rearrange("p i u q -> p i q u"),
             )
@@ -253,15 +257,12 @@ def tile_encoderlayer_pa_kernel(tc, q, k, v, out):
             nc.vector.reciprocal(out=inverse[:], in_=state["row_sum"][:])
             state["inverse"] = inverse
 
-        def weighted_sum_and_store(step):
+        def weighted_sums(step):
             state = in_flight[step]
-            t = state["t"]
             g = state["window"]
-            first_head = state["first_head"]
             o_ps = psum.tile([P, PAIR, FEAT], F32, tag="o_ps", bufs=1)
-            o_sb = work.tile([P, PAIR, FEAT], F32, tag="o_sb", bufs=4)
             for i in range(PAIR):
-                h = first_head + i
+                h = state["first_head"] + i
                 queries = slice(i * P, (i + 1) * P)
                 cols = slice(h * FEAT, (h + 1) * FEAT)
                 nc.tensor.matmul_mx(
@@ -272,11 +273,17 @@ def tile_encoderlayer_pa_kernel(tc, q, k, v, out):
                     rhs_scale=v_scales[g][:, cols],
                     start=True, stop=True,
                 )
-            for i in range(PAIR):
-                nc.scalar.activation(
-                    out=o_sb[:, i, :], in_=o_ps[:, i, :], func=ACT.Copy,
-                    scale=state["inverse"][:, i : i + 1],
-                )
+            state["o_ps"] = o_ps
+
+        def divide_and_store(step):
+            state = in_flight[step]
+            t = state["t"]
+            first_head = state["first_head"]
+            o_sb = work.tile([P, PAIR, FEAT], F32, tag="o_sb", bufs=4)
+            nc.vector.tensor_tensor(
+                out=o_sb[:], in0=state["o_ps"][:],
+                in1=state["inverse"][:].unsqueeze(2).to_broadcast([P, PAIR, FEAT]), op=ALU.mult,
+            )
             nc.sync.dma_start(
                 out=out_rows[t * P : (t + 1) * P, first_head * FEAT : (first_head + PAIR) * FEAT],
                 in_=o_sb[:].rearrange("q i f -> q (i f)"),
@@ -285,10 +292,18 @@ def tile_encoderlayer_pa_kernel(tc, q, k, v, out):
         def transposes_ahead(step):
             t = step // STEPS_PER_TILE
             part = step % STEPS_PER_TILE
-            if part < 2 and t + 1 < TILES:
-                transpose_q(t + 1, part, True)
-            if part >= 2 and 3 <= t + 2 < TILES:
-                transpose_k(t + 2, part - 2, True)
+            if step == 0:
+                transpose_q(0, 1, True)
+                transpose_k(0, 1, True)
+            elif step == 1:
+                transpose_k(1, 1, True)
+                transpose_k(2, 1, True)
+            elif t == 0:
+                transpose_q(1, part - 2, True)
+            elif part % 2 == 0 and t + 1 < TILES:
+                transpose_q(t + 1, part // 2, True)
+            elif part % 2 == 1 and t + 2 < TILES:
+                transpose_k(t + 2, part // 2, True)
 
         def loads_ahead(t):
             for half in range(2):
@@ -297,9 +312,9 @@ def tile_encoderlayer_pa_kernel(tc, q, k, v, out):
             for half in range(2):
                 if t + 4 < TILES:
                     load_k(t + 4, half)
-            for half in range(2):
+            for pair in range(STEPS_PER_TILE):
                 if t % 2 == 1 and (t + 3) // 2 < GROUPS:
-                    load_v((t + 3) // 2, half)
+                    load_v((t + 3) // 2, pair)
 
         stack.enter_context(tc.manual_schedule())
         for half in range(2):
@@ -307,36 +322,43 @@ def tile_encoderlayer_pa_kernel(tc, q, k, v, out):
             for t in range(3):
                 load_k(t, half)
             load_v(0, half)
+        load_v(0, 2)
+        load_v(0, 3)
         for half in range(2):
             load_q(1, half)
         for half in range(2):
             load_k(3, half)
-        for half in range(2):
-            load_v(1, half)
-        for half in range(2):
-            transpose_q(0, half, True)
-            for t in range(3):
-                transpose_k(t, half, t % 2 == 1)
+        for pair in range(STEPS_PER_TILE):
+            load_v(1, pair)
+        transpose_q(0, 0, True)
+        for t in range(3):
+            transpose_k(t, 0, t % 2 == 1)
+        for chunk in range(V_AHEAD):
+            regroup_v(chunk)
 
+        next_chunk = 0
         for step in range(STEPS + 3):
             if 0 <= step - 3:
                 quantise_e(step - 3)
+            first_chunk = next_chunk
+            while next_chunk < CHUNKS and max(next_chunk // 2 + 3, next_chunk - 1) <= step:
+                quantise_v(next_chunk)
+                next_chunk += 1
+            for chunk in range(first_chunk + V_AHEAD, min(next_chunk + V_AHEAD, CHUNKS)):
+                regroup_v(chunk)
+            if 0 <= step - 3:
+                invert_row_sums(step - 3)
             if 0 <= step - 2 < STEPS:
                 transpose_e(step - 2)
             if step < STEPS:
                 if step % STEPS_PER_TILE == 0:
                     loads_ahead(step // STEPS_PER_TILE)
                 transposes_ahead(step)
-            v_heads = v_heads_of(step)
-            v_grouped_tiles = [regroup_v(g, h) for (g, h) in v_heads]
-            if step < STEPS:
                 begin(step)
                 scores(step, 0)
-            for (g, h), v_grouped_tile in zip(v_heads, v_grouped_tiles):
-                quantise_v(g, h, v_grouped_tile)
             if 0 <= step - 3:
-                invert_row_sums(step - 3)
-                weighted_sum_and_store(step - 3)
+                weighted_sums(step - 3)
+                divide_and_store(step - 3)
             if step < STEPS:
                 scores(step, 1)
                 exponentials(step)

@@ -316,7 +316,6 @@ def tile_encoderlayer_pa_kernel(tc, q, k, v, out):
                 if t % 2 == 1 and (t + 3) // 2 < GROUPS:
                     load_v((t + 3) // 2, pair)
 
-        stack.enter_context(tc.manual_schedule())
         for half in range(2):
             load_q(0, half)
             for t in range(3):

@@ -316,6 +316,7 @@ def tile_encoderlayer_pa_kernel(tc, q, k, v, out):
                 if t % 2 == 1 and (t + 3) // 2 < GROUPS:
                     load_v((t + 3) // 2, pair)
 
+        stack.enter_context(tc.manual_schedule())
         for half in range(2):
             load_q(0, half)
             for t in range(3):
@@ -337,14 +338,14 @@ def tile_encoderlayer_pa_kernel(tc, q, k, v, out):
 
         next_chunk = 0
         for step in range(STEPS + 3):
-            if 0 <= step - 3:
-                quantise_e(step - 3)
             first_chunk = next_chunk
             while next_chunk < CHUNKS and max(next_chunk // 2 + 3, next_chunk - 1) <= step:
                 quantise_v(next_chunk)
                 next_chunk += 1
             for chunk in range(first_chunk + V_AHEAD, min(next_chunk + V_AHEAD, CHUNKS)):
                 regroup_v(chunk)
+            if 0 <= step - 3:
+                quantise_e(step - 3)
             if 0 <= step - 3:
                 invert_row_sums(step - 3)
             if 0 <= step - 2 < STEPS:

@@ -1,3 +1,4 @@
+import math
 from contextlib import ExitStack
 
 import concourse.mybir as mybir
@@ -173,13 +174,13 @@ def tile_encoderlayer_pa_kernel(tc, q, k, v, out):
             t = step // STEPS_PER_TILE
             first_key_tile = clamp(t - 1, 0, TILES - 3)
             window = clamp((t - 1) // 2, 0, GROUPS - 1)
-            shift = stats.tile([P, PAIR], F32, tag="shift")
+            peak = stats.tile([P, PAIR], F32, tag="peak")
             row_sum = stats.tile([P, PAIR], F32, tag="row_sum")
             in_flight[step] = {
                 "t": t, "first_head": PAIR * (step % STEPS_PER_TILE),
                 "first_key_tile": first_key_tile, "window": window,
                 "quarter": first_key_tile - 2 * window,
-                "shift": shift, "row_sum": row_sum, "banks": [],
+                "peak": peak, "row_sum": row_sum, "banks": [],
             }
 
         def scores(step, i):
@@ -205,23 +206,29 @@ def tile_encoderlayer_pa_kernel(tc, q, k, v, out):
                 lhsT=ident_bf[:], rhs=mask_bf[:, first_mask : first_mask + 2, :],
                 start=False, stop=True,
             )
-            unused = work.tile([P, SPAN], F32, tag="unused", bufs=4)
-            nc.vector.tensor_scalar(
-                out=unused[:], in0=s_ps[:], scalar1=-SCALE, scalar2=None, op0=ALU.mult, op1=ALU.min,
-                accum_out=state["shift"][:, i : i + 1],
-            )
+            nc.vector.tensor_reduce(out=state["peak"][:, i : i + 1], in_=s_ps[:], axis=AXIS.X, op=ALU.max)
             state["banks"].append(s_ps)
+
+        def shifts(step):
+            state = in_flight[step]
+            moved = stats.tile([P, PAIR], F32, tag="moved")
+            nc.vector.tensor_scalar(
+                out=moved[:], in0=state["peak"][:], scalar1=-SCALE, scalar2=math.log(2.0),
+                op0=ALU.mult, op1=ALU.add,
+            )
+            state["moved"] = moved
 
         def exponentials(step):
             state = in_flight[step]
             quarter = state["quarter"]
+            moved = state["moved"]
             for i in range(PAIR):
                 h = state["first_head"] + i
                 e_view = e_tiles[quarter][:, h, :].rearrange("q (u b x) -> q b u x", u=2, b=4)
                 nc.scalar.activation(
                     out=e_view[:, quarter : quarter + 3, :, :],
                     in_=state["banks"][i][:].rearrange("q (b u x) -> q b u x", b=3, u=2),
-                    func=ACT.Exp, bias=state["shift"][:, i : i + 1], scale=SCALE,
+                    func=ACT.Exp, bias=moved[:, i : i + 1], scale=SCALE,
                     accum_out=state["row_sum"][:, i : i + 1],
                 )
 
@@ -336,29 +343,36 @@ def tile_encoderlayer_pa_kernel(tc, q, k, v, out):
         for chunk in range(V_AHEAD):
             regroup_v(chunk)
 
+        def live(step):
+            return 0 <= step < STEPS
+
         next_chunk = 0
-        for step in range(STEPS + 3):
+        for rnd in range(STEPS + 6):
+            if live(rnd):
+                if rnd % STEPS_PER_TILE == 0:
+                    loads_ahead(rnd // STEPS_PER_TILE)
+                begin(rnd)
+                scores(rnd, 0)
+            if live(rnd - 5):
+                weighted_sums(rnd - 5)
+                divide_and_store(rnd - 5)
+            if live(rnd):
+                scores(rnd, 1)
+            if live(rnd - 1):
+                exponentials(rnd - 1)
+            if live(rnd - 2):
+                transpose_e(rnd - 2)
+            if live(rnd):
+                transposes_ahead(rnd)
+            if live(rnd - 3):
+                quantise_e(rnd - 3)
             first_chunk = next_chunk
-            while next_chunk < CHUNKS and max(next_chunk // 2 + 3, next_chunk - 1) <= step:
+            while next_chunk < CHUNKS and max(next_chunk // 2 + 2, next_chunk - 1) <= rnd:
                 quantise_v(next_chunk)
                 next_chunk += 1
             for chunk in range(first_chunk + V_AHEAD, min(next_chunk + V_AHEAD, CHUNKS)):
                 regroup_v(chunk)
-            if 0 <= step - 3:
-                quantise_e(step - 3)
-            if 0 <= step - 3:
-                invert_row_sums(step - 3)
-            if 0 <= step - 2 < STEPS:
-                transpose_e(step - 2)
-            if step < STEPS:
-                if step % STEPS_PER_TILE == 0:
-                    loads_ahead(step // STEPS_PER_TILE)
-                transposes_ahead(step)
-                begin(step)
-                scores(step, 0)
-            if 0 <= step - 3:
-                weighted_sums(step - 3)
-                divide_and_store(step - 3)
-            if step < STEPS:
-                scores(step, 1)
-                exponentials(step)
+            if live(rnd):
+                shifts(rnd)
+            if live(rnd - 1):
+                invert_row_sums(rnd - 1)

@@ -8,6 +8,7 @@ F32 = mybir.dt.float32
 BF16 = mybir.dt.bfloat16
 U32 = mybir.dt.uint32
 U8 = mybir.dt.uint8
+I32 = mybir.dt.int32
 FP8X4 = mybir.dt.float8_e4m3fn_x4
 ALU = mybir.AluOpType
 ACT = mybir.ActivationFunctionType
@@ -26,7 +27,8 @@ PAIR = 2
 STEPS_PER_TILE = HEADS // PAIR
 STEPS = TILES * STEPS_PER_TILE
 GROUPS = 5
-CHUNKS = GROUPS * HEADS
+OWN_WINDOWS = 3
+CHUNKS = OWN_WINDOWS * HEADS
 V_AHEAD = 4
 SCALE = 1.0 / 16.0
 MASKED = -1.0e9 / SCALE
@@ -91,12 +93,20 @@ def tile_encoderlayer_pa_kernel(tc, q, k, v, out):
         kT_words = kT[:].bitcast(F32)
         kT_feat = kT[:].rearrange("p h (s e) -> p h s e", e=2)
 
+        v_codes = {}
+        v_scales = {}
+        for g in range(GROUPS):
+            codes = const.tile([P, ROW], U32, name="codes%d" % g, align_bytes=64)
+            scales = const.tile([P, ROW], U8, name="scales%d" % g, align_bytes=64)
+            v_codes[g] = codes
+            v_scales[g] = scales
+            if g % 2 == 0:
+                nc.vector.memset(scales[:].bitcast(I32), 0)
+
         q_sb = {}
         k_sb = {}
         v_raw = {}
         qT = {}
-        v_codes = {}
-        v_scales = {}
         in_flight = {}
         v_grouped_tiles = {}
 
@@ -114,12 +124,8 @@ def tile_encoderlayer_pa_kernel(tc, q, k, v, out):
 
         def load_v(g, pair):
             if pair == 0:
-                v_tile = loads.tile([P, PACK, ROW], BF16, tag="v_tile", bufs=3)
-                codes = work.tile([P, ROW], U32, tag="v_codes", align_bytes=64)
-                scales = work.tile([P, ROW], U8, tag="v_scales", align_bytes=64)
+                v_tile = loads.tile([P, PACK, ROW], BF16, tag="v_tile", bufs=2)
                 v_raw[g] = v_tile
-                v_codes[g] = codes
-                v_scales[g] = scales
             first = 2 * g * P
             cols = slice(pair * PAIR * FEAT, (pair + 1) * PAIR * FEAT)
             nc.sync.dma_start(
@@ -152,7 +158,7 @@ def tile_encoderlayer_pa_kernel(tc, q, k, v, out):
             transpose_four_heads(k_sb[(t, half)], key_order, dest, on_scalar)
 
         def regroup_v(chunk):
-            g, h = chunk // HEADS, chunk % HEADS
+            g, h = 2 * (chunk // HEADS), chunk % HEADS
             v_grouped = work.tile([P, FEAT, PACK], BF16, tag="v_grouped", bufs=V_AHEAD, align_bytes=64)
             nc.gpsimd.tensor_scalar(
                 out=v_grouped[:],
@@ -162,13 +168,23 @@ def tile_encoderlayer_pa_kernel(tc, q, k, v, out):
             v_grouped_tiles[chunk] = v_grouped
 
         def quantise_v(chunk):
-            g, h = chunk // HEADS, chunk % HEADS
+            g, h = 2 * (chunk // HEADS), chunk % HEADS
             cols = slice(h * FEAT, (h + 1) * FEAT)
             nc.vector.quantize_mx(
                 out=v_codes[g][:, cols].bitcast(FP8X4),
                 scales=v_scales[g][:, cols],
                 in_=v_grouped_tiles[chunk][:].rearrange("p w j -> p (w j)"),
             )
+
+        def copy_window(g, half):
+            cols = slice(half * (ROW // 2), (half + 1) * (ROW // 2))
+            for tiles in (v_codes, v_scales):
+                nc.sync.dma_start(
+                    out=tiles[g][0 : P // 2, cols].bitcast(I32), in_=tiles[g - 1][P // 2 : P, cols].bitcast(I32),
+                )
+                nc.sync.dma_start(
+                    out=tiles[g][P // 2 : P, cols].bitcast(I32), in_=tiles[g + 1][0 : P // 2, cols].bitcast(I32),
+                )
 
         def begin(step):
             t = step // STEPS_PER_TILE
@@ -320,8 +336,8 @@ def tile_encoderlayer_pa_kernel(tc, q, k, v, out):
                 if t + 4 < TILES:
                     load_k(t + 4, half)
             for pair in range(STEPS_PER_TILE):
-                if t % 2 == 1 and (t + 3) // 2 < GROUPS:
-                    load_v((t + 3) // 2, pair)
+                if t == 2:
+                    load_v(4, pair)
 
         stack.enter_context(tc.manual_schedule())
         for half in range(2):
@@ -336,7 +352,7 @@ def tile_encoderlayer_pa_kernel(tc, q, k, v, out):
         for half in range(2):
             load_k(3, half)
         for pair in range(STEPS_PER_TILE):
-            load_v(1, pair)
+            load_v(2, pair)
         transpose_q(0, 0, True)
         for t in range(3):
             transpose_k(t, 0, t % 2 == 1)
@@ -345,6 +361,11 @@ def tile_encoderlayer_pa_kernel(tc, q, k, v, out):
 
         def live(step):
             return 0 <= step < STEPS
+
+        def chunk_round(chunk):
+            if chunk < 2 * HEADS:
+                return max(chunk // 2 + 2, chunk - 1)
+            return 2 * chunk - 17
 
         next_chunk = 0
         for rnd in range(STEPS + 6):
@@ -367,8 +388,10 @@ def tile_encoderlayer_pa_kernel(tc, q, k, v, out):
             if live(rnd - 3):
                 quantise_e(rnd - 3)
             first_chunk = next_chunk
-            while next_chunk < CHUNKS and max(next_chunk // 2 + 2, next_chunk - 1) <= rnd:
+            while next_chunk < CHUNKS and chunk_round(next_chunk) <= rnd:
                 quantise_v(next_chunk)
+                if next_chunk >= HEADS and next_chunk % 4 == 3:
+                    copy_window(2 * (next_chunk // HEADS) - 1, (next_chunk % HEADS) // 4)
                 next_chunk += 1
             for chunk in range(first_chunk + V_AHEAD, min(next_chunk + V_AHEAD, CHUNKS)):
                 regroup_v(chunk)

@@ -364,8 +364,8 @@ def tile_encoderlayer_pa_kernel(tc, q, k, v, out):
 
         def chunk_round(chunk):
             if chunk < 2 * HEADS:
-                return max(chunk // 2 + 2, chunk - 1)
-            return 2 * chunk - 17
+                return chunk
+            return 2 * chunk - 15
 
         next_chunk = 0
         for rnd in range(STEPS + 6):
@@ -385,8 +385,6 @@ def tile_encoderlayer_pa_kernel(tc, q, k, v, out):
                 transpose_e(rnd - 2)
             if live(rnd):
                 transposes_ahead(rnd)
-            if live(rnd - 3):
-                quantise_e(rnd - 3)
             first_chunk = next_chunk
             while next_chunk < CHUNKS and chunk_round(next_chunk) <= rnd:
                 quantise_v(next_chunk)
@@ -395,6 +393,8 @@ def tile_encoderlayer_pa_kernel(tc, q, k, v, out):
                 next_chunk += 1
             for chunk in range(first_chunk + V_AHEAD, min(next_chunk + V_AHEAD, CHUNKS)):
                 regroup_v(chunk)
+            if live(rnd - 3):
+                quantise_e(rnd - 3)
             if live(rnd):
                 shifts(rnd)
             if live(rnd - 1):

@@ -141,7 +141,7 @@ def tile_encoderlayer_pa_kernel(tc, q, k, v, out):
 
         def transpose_four_heads(half_tile, order, dest, on_scalar):
             words = half_tile[:].bitcast(F32)
-            turned = psum.tile([P, 4, P], F32, tag="turned", bufs=3)
+            turned = psum.tile([P, 4, P], F32, tag="turned", bufs=2)
             for i in range(4):
                 nc.tensor.transpose(turned[:, i, :], words[:, i * P : (i + 1) * P], order[:])
             copy_out(on_scalar, dest, turned[:])
@@ -211,7 +211,7 @@ def tile_encoderlayer_pa_kernel(tc, q, k, v, out):
                 masked_tiles, first_mask = slice(0, 3, 2), 1
             keys = slice(state["first_key_tile"] * P, state["first_key_tile"] * P + SPAN)
             qT_feat = qT[t][:].rearrange("p h (r e) -> p h r e", e=2)
-            s_ps = psum.tile([P, SPAN], F32, tag="s_ps", bufs=4)
+            s_ps = psum.tile([P, SPAN], F32, tag="s_ps", bufs=5)
             for e in range(2):
                 nc.tensor.matmul(
                     out=s_ps[:], lhsT=qT_feat[:, h, :, e], rhs=kT_feat[:, h, keys, e],
@@ -251,7 +251,7 @@ def tile_encoderlayer_pa_kernel(tc, q, k, v, out):
         def transpose_e(step):
             state = in_flight[step]
             e_words = e_tiles[state["quarter"]][:].bitcast(F32)
-            turned = psum.tile([P, PAIR, 2, P], F32, tag="turned", bufs=3)
+            turned = psum.tile([P, PAIR, 2, P], F32, tag="turned", bufs=2)
             for i in range(PAIR):
                 h = state["first_head"] + i
                 for u in range(2):

@@ -108,6 +108,8 @@ def tile_encoderlayer_pa_kernel(tc, q, k, v, out):
         v_raw = {}
         qT = {}
         in_flight = {}
+        tile_sums = {}
+        tile_inverse = {}
         v_grouped_tiles = {}
 
         def load_rows(rows, t, half, tag, bufs):
@@ -191,12 +193,14 @@ def tile_encoderlayer_pa_kernel(tc, q, k, v, out):
             first_key_tile = clamp(t - 1, 0, TILES - 3)
             window = clamp((t - 1) // 2, 0, GROUPS - 1)
             peak = stats.tile([P, PAIR], F32, tag="peak")
-            row_sum = stats.tile([P, PAIR], F32, tag="row_sum")
+            if step % STEPS_PER_TILE == 0:
+                row_sums = stats.tile([P, HEADS], F32, tag="row_sums")
+                tile_sums[t] = row_sums
             in_flight[step] = {
                 "t": t, "first_head": PAIR * (step % STEPS_PER_TILE),
                 "first_key_tile": first_key_tile, "window": window,
                 "quarter": first_key_tile - 2 * window,
-                "peak": peak, "row_sum": row_sum, "banks": [],
+                "peak": peak, "banks": [],
             }
 
         def scores(step, i):
@@ -228,7 +232,7 @@ def tile_encoderlayer_pa_kernel(tc, q, k, v, out):
         def shifts(step):
             state = in_flight[step]
             moved = stats.tile([P, PAIR], F32, tag="moved")
-            nc.vector.tensor_scalar(
+            nc.gpsimd.tensor_scalar(
                 out=moved[:], in0=state["peak"][:], scalar1=-SCALE, scalar2=math.log(2.0),
                 op0=ALU.mult, op1=ALU.add,
             )
@@ -245,7 +249,7 @@ def tile_encoderlayer_pa_kernel(tc, q, k, v, out):
                     out=e_view[:, quarter : quarter + 3, :, :],
                     in_=state["banks"][i][:].rearrange("q (b u x) -> q b u x", b=3, u=2),
                     func=ACT.Exp, bias=moved[:, i : i + 1], scale=SCALE,
-                    accum_out=state["row_sum"][:, i : i + 1],
+                    accum_out=tile_sums[state["t"]][:, h : h + 1],
                 )
 
         def transpose_e(step):
@@ -274,11 +278,10 @@ def tile_encoderlayer_pa_kernel(tc, q, k, v, out):
             state["e_codes"] = e_codes
             state["e_scales"] = e_scales
 
-        def invert_row_sums(step):
-            state = in_flight[step]
-            inverse = stats.tile([P, PAIR], F32, tag="inverse")
-            nc.vector.reciprocal(out=inverse[:], in_=state["row_sum"][:])
-            state["inverse"] = inverse
+        def invert_row_sums(t):
+            inverse = stats.tile([P, HEADS], F32, tag="inverse")
+            nc.vector.reciprocal(out=inverse[:], in_=tile_sums[t][:])
+            tile_inverse[t] = inverse
 
         def weighted_sums(step):
             state = in_flight[step]
@@ -305,7 +308,8 @@ def tile_encoderlayer_pa_kernel(tc, q, k, v, out):
             o_sb = work.tile([P, PAIR, FEAT], F32, tag="o_sb", bufs=4)
             nc.vector.tensor_tensor(
                 out=o_sb[:], in0=state["o_ps"][:],
-                in1=state["inverse"][:].unsqueeze(2).to_broadcast([P, PAIR, FEAT]), op=ALU.mult,
+                in1=tile_inverse[t][:, first_head : first_head + PAIR].unsqueeze(2).to_broadcast([P, PAIR, FEAT]),
+                op=ALU.mult,
             )
             nc.sync.dma_start(
                 out=out_rows[t * P : (t + 1) * P, first_head * FEAT : (first_head + PAIR) * FEAT],
@@ -379,6 +383,7 @@ def tile_encoderlayer_pa_kernel(tc, q, k, v, out):
                 divide_and_store(rnd - 5)
             if live(rnd):
                 scores(rnd, 1)
+                shifts(rnd)
             if live(rnd - 1):
                 exponentials(rnd - 1)
             if live(rnd - 2):
@@ -395,7 +400,5 @@ def tile_encoderlayer_pa_kernel(tc, q, k, v, out):
                 regroup_v(chunk)
             if live(rnd - 3):
                 quantise_e(rnd - 3)
-            if live(rnd):
-                shifts(rnd)
-            if live(rnd - 1):
-                invert_row_sums(rnd - 1)
+            if live(rnd - 1) and rnd % STEPS_PER_TILE == 0:
+                invert_row_sums((rnd - 1) // STEPS_PER_TILE)

@@ -143,7 +143,7 @@ def tile_encoderlayer_pa_kernel(tc, q, k, v, out):
 
         def transpose_four_heads(half_tile, order, dest, on_scalar):
             words = half_tile[:].bitcast(F32)
-            turned = psum.tile([P, 4, P], F32, tag="turned", bufs=2)
+            turned = psum.tile([P, 4, P], F32, tag="turned", bufs=3)
             for i in range(4):
                 nc.tensor.transpose(turned[:, i, :], words[:, i * P : (i + 1) * P], order[:])
             copy_out(on_scalar, dest, turned[:])
@@ -215,7 +215,7 @@ def tile_encoderlayer_pa_kernel(tc, q, k, v, out):
                 masked_tiles, first_mask = slice(0, 3, 2), 1
             keys = slice(state["first_key_tile"] * P, state["first_key_tile"] * P + SPAN)
             qT_feat = qT[t][:].rearrange("p h (r e) -> p h r e", e=2)
-            s_ps = psum.tile([P, SPAN], F32, tag="s_ps", bufs=5)
+            s_ps = psum.tile([P, SPAN], F32, tag="s_ps", bufs=3)
             for e in range(2):
                 nc.tensor.matmul(
                     out=s_ps[:], lhsT=qT_feat[:, h, :, e], rhs=kT_feat[:, h, keys, e],
@@ -226,14 +226,18 @@ def tile_encoderlayer_pa_kernel(tc, q, k, v, out):
                 lhsT=ident_bf[:], rhs=mask_bf[:, first_mask : first_mask + 2, :],
                 start=False, stop=True,
             )
-            nc.vector.tensor_reduce(out=state["peak"][:, i : i + 1], in_=s_ps[:], axis=AXIS.X, op=ALU.max)
-            state["banks"].append(s_ps)
+            minus_s = work.tile([P, SPAN], F32, tag="minus_s", bufs=6)
+            nc.vector.tensor_scalar(
+                out=minus_s[:], in0=s_ps[:], scalar1=-SCALE, scalar2=None, op0=ALU.mult, op1=ALU.min,
+                accum_out=state["peak"][:, i : i + 1],
+            )
+            state["banks"].append(minus_s)
 
         def shifts(step):
             state = in_flight[step]
             moved = stats.tile([P, PAIR], F32, tag="moved")
             nc.gpsimd.tensor_scalar(
-                out=moved[:], in0=state["peak"][:], scalar1=-SCALE, scalar2=math.log(2.0),
+                out=moved[:], in0=state["peak"][:], scalar1=1.0, scalar2=math.log(2.0),
                 op0=ALU.mult, op1=ALU.add,
             )
             state["moved"] = moved
@@ -248,14 +252,14 @@ def tile_encoderlayer_pa_kernel(tc, q, k, v, out):
                 nc.scalar.activation(
                     out=e_view[:, quarter : quarter + 3, :, :],
                     in_=state["banks"][i][:].rearrange("q (b u x) -> q b u x", b=3, u=2),
-                    func=ACT.Exp, bias=moved[:, i : i + 1], scale=SCALE,
+                    func=ACT.Exp, bias=moved[:, i : i + 1], scale=-1.0,
                     accum_out=tile_sums[state["t"]][:, h : h + 1],
                 )
 
         def transpose_e(step):
             state = in_flight[step]
             e_words = e_tiles[state["quarter"]][:].bitcast(F32)
-            turned = psum.tile([P, PAIR, 2, P], F32, tag="turned", bufs=2)
+            turned = psum.tile([P, PAIR, 2, P], F32, tag="turned", bufs=3)
             for i in range(PAIR):
                 h = state["first_head"] + i
                 for u in range(2):
@@ -286,7 +290,7 @@ def tile_encoderlayer_pa_kernel(tc, q, k, v, out):
         def weighted_sums(step):
             state = in_flight[step]
             g = state["window"]
-            o_ps = psum.tile([P, PAIR, FEAT], F32, tag="o_ps", bufs=1)
+            o_ps = psum.tile([P, PAIR, FEAT], F32, tag="o_ps", bufs=2)
             for i in range(PAIR):
                 h = state["first_head"] + i
                 queries = slice(i * P, (i + 1) * P)

@@ -59,16 +59,14 @@ def tile_encoderlayer_pa_kernel(tc, q, k, v, out):
         ident_bf = const.tile([P, P], BF16)
         make_identity(nc, ident_bf[:])
 
-        mask_f32 = const.tile([P, 4, P], F32)
-        nc.gpsimd.memset(mask_f32[:, 0, :], MASKED)
-        nc.gpsimd.memset(mask_f32[:, 1:3, :], 0.0)
-        nc.gpsimd.memset(mask_f32[:, 3, :], MASKED)
+        mask_f32 = const.tile([P, 2, P], F32)
+        nc.gpsimd.memset(mask_f32[:], 0.0)
         nc.gpsimd.affine_select(
-            out=mask_f32[:, 1, :], in_=mask_f32[:, 1, :], compare_op=ALU.is_ge, fill=MASKED,
+            out=mask_f32[:, 0, :], in_=mask_f32[:, 0, :], compare_op=ALU.is_ge, fill=MASKED,
             base=0, pattern=[[1, P]], channel_multiplier=-1,
         )
         nc.gpsimd.affine_select(
-            out=mask_f32[:, 2, :], in_=mask_f32[:, 2, :], compare_op=ALU.is_ge, fill=MASKED,
+            out=mask_f32[:, 1, :], in_=mask_f32[:, 1, :], compare_op=ALU.is_ge, fill=MASKED,
             base=0, pattern=[[-1, P]], channel_multiplier=1,
         )
         key_order = const.tile([P, P], F32)
@@ -76,8 +74,8 @@ def tile_encoderlayer_pa_kernel(tc, q, k, v, out):
             out=key_order[:].rearrange("i (u c e) -> i u c e", u=2, e=2),
             in_=ident_f32[:].rearrange("i (c u e) -> i u c e", u=2, e=2),
         )
-        mask_bf = const.tile([P, 4, P], BF16)
-        for block in range(4):
+        mask_bf = const.tile([P, 2, P], BF16)
+        for block in range(2):
             nc.vector.tensor_copy(
                 out=mask_bf[:, block, :].rearrange("q (u c e) -> q u c e", u=2, e=2),
                 in_=mask_f32[:, block, :].rearrange("q (c u e) -> q u c e", u=2, e=2),
@@ -85,9 +83,11 @@ def tile_encoderlayer_pa_kernel(tc, q, k, v, out):
 
         e_low = const.tile([P, HEADS, K_PASS], BF16)
         e_high = const.tile([P, HEADS, K_PASS], BF16)
-        e_tiles = [e_low, e_high]
-        nc.vector.memset(e_low[:].rearrange("q h (u c) -> q (h u) c", u=2)[:, :, 192:256], 0.0)
+        e_last = const.tile([P, HEADS, K_PASS], BF16)
+        e_tiles = [e_low, e_high, e_last]
+        nc.vector.memset(e_low[:].rearrange("q h (u c) -> q (h u) c", u=2)[:, :, 128:256], 0.0)
         nc.vector.memset(e_high[:].rearrange("q h (u c) -> q (h u) c", u=2)[:, :, 0:64], 0.0)
+        nc.gpsimd.memset(e_last[:].rearrange("q h (u c) -> q (h u) c", u=2)[:, :, 0:128], 0.0)
 
         kT = const.tile([P, HEADS, SEQ * 2], BF16)
         kT_words = kT[:].bitcast(F32)
@@ -190,7 +190,8 @@ def tile_encoderlayer_pa_kernel(tc, q, k, v, out):
 
         def begin(step):
             t = step // STEPS_PER_TILE
-            first_key_tile = clamp(t - 1, 0, TILES - 3)
+            first_key_tile = max(t - 1, 0)
+            key_tiles = min(t + 1, TILES - 1) - first_key_tile + 1
             window = clamp((t - 1) // 2, 0, GROUPS - 1)
             peak = stats.tile([P, PAIR], F32, tag="peak")
             if step % STEPS_PER_TILE == 0:
@@ -199,6 +200,7 @@ def tile_encoderlayer_pa_kernel(tc, q, k, v, out):
             in_flight[step] = {
                 "t": t, "first_head": PAIR * (step % STEPS_PER_TILE),
                 "first_key_tile": first_key_tile, "window": window,
+                "key_tiles": key_tiles,
                 "quarter": first_key_tile - 2 * window,
                 "peak": peak, "banks": [],
             }
@@ -208,27 +210,28 @@ def tile_encoderlayer_pa_kernel(tc, q, k, v, out):
             t = state["t"]
             h = state["first_head"] + i
             if t == 0:
-                masked_tiles, first_mask = slice(1, 3), 2
+                masked_tiles, blocks = slice(1, 2), slice(1, 2)
             elif t == TILES - 1:
-                masked_tiles, first_mask = slice(0, 2), 0
+                masked_tiles, blocks = slice(0, 1), slice(0, 1)
             else:
-                masked_tiles, first_mask = slice(0, 3, 2), 1
-            keys = slice(state["first_key_tile"] * P, state["first_key_tile"] * P + SPAN)
+                masked_tiles, blocks = slice(0, 3, 2), slice(0, 2)
+            span = state["key_tiles"] * P
+            keys = slice(state["first_key_tile"] * P, state["first_key_tile"] * P + span)
             qT_feat = qT[t][:].rearrange("p h (r e) -> p h r e", e=2)
             s_ps = psum.tile([P, SPAN], F32, tag="s_ps", bufs=3)
             for e in range(2):
                 nc.tensor.matmul(
-                    out=s_ps[:], lhsT=qT_feat[:, h, :, e], rhs=kT_feat[:, h, keys, e],
+                    out=s_ps[:, 0:span], lhsT=qT_feat[:, h, :, e], rhs=kT_feat[:, h, keys, e],
                     start=(e == 0), stop=False,
                 )
             nc.tensor.matmul(
                 out=s_ps[:].rearrange("q (b c) -> q b c", c=P)[:, masked_tiles, :],
-                lhsT=ident_bf[:], rhs=mask_bf[:, first_mask : first_mask + 2, :],
+                lhsT=ident_bf[:], rhs=mask_bf[:, blocks, :],
                 start=False, stop=True,
             )
             minus_s = work.tile([P, SPAN], F32, tag="minus_s", bufs=6)
             nc.vector.tensor_scalar(
-                out=minus_s[:], in0=s_ps[:], scalar1=-SCALE, scalar2=None, op0=ALU.mult, op1=ALU.min,
+                out=minus_s[:, 0:span], in0=s_ps[:, 0:span], scalar1=-SCALE, scalar2=None, op0=ALU.mult, op1=ALU.min,
                 accum_out=state["peak"][:, i : i + 1],
             )
             state["banks"].append(minus_s)
@@ -245,13 +248,14 @@ def tile_encoderlayer_pa_kernel(tc, q, k, v, out):
         def exponentials(step):
             state = in_flight[step]
             quarter = state["quarter"]
+            key_tiles = state["key_tiles"]
             moved = state["moved"]
             for i in range(PAIR):
                 h = state["first_head"] + i
                 e_view = e_tiles[quarter][:, h, :].rearrange("q (u b x) -> q b u x", u=2, b=4)
                 nc.scalar.activation(
-                    out=e_view[:, quarter : quarter + 3, :, :],
-                    in_=state["banks"][i][:].rearrange("q (b u x) -> q b u x", b=3, u=2),
+                    out=e_view[:, quarter : quarter + key_tiles, :, :],
+                    in_=state["banks"][i][:, 0 : key_tiles * P].rearrange("q (b u x) -> q b u x", b=key_tiles, u=2),
                     func=ACT.Exp, bias=moved[:, i : i + 1], scale=-1.0,
                     accum_out=tile_sums[state["t"]][:, h : h + 1],
                 )
@@ -328,9 +332,12 @@ def tile_encoderlayer_pa_kernel(tc, q, k, v, out):
                 transpose_k(0, 1, True)
             elif step == 1:
                 transpose_k(1, 1, True)
+                transpose_k(2, 0, True)
+            elif step == 2:
+                transpose_q(1, 0, True)
                 transpose_k(2, 1, True)
-            elif t == 0:
-                transpose_q(1, part - 2, True)
+            elif step == 3:
+                transpose_q(1, 1, True)
             elif part % 2 == 0 and t + 1 < TILES:
                 transpose_q(t + 1, part // 2, True)
             elif part % 2 == 1 and t + 2 < TILES:
@@ -350,11 +357,13 @@ def tile_encoderlayer_pa_kernel(tc, q, k, v, out):
         stack.enter_context(tc.manual_schedule())
         for half in range(2):
             load_q(0, half)
-            for t in range(3):
+            for t in range(2):
                 load_k(t, half)
             load_v(0, half)
         load_v(0, 2)
         load_v(0, 3)
+        for half in range(2):
+            load_k(2, half)
         for half in range(2):
             load_q(1, half)
         for half in range(2):
@@ -362,7 +371,7 @@ def tile_encoderlayer_pa_kernel(tc, q, k, v, out):
         for pair in range(STEPS_PER_TILE):
             load_v(2, pair)
         transpose_q(0, 0, True)
-        for t in range(3):
+        for t in range(2):
             transpose_k(t, 0, t % 2 == 1)
         for chunk in range(V_AHEAD):
             regroup_v(chunk)

@@ -54,6 +54,10 @@ def tile_encoderlayer_pa_kernel(tc, q, k, v, out):
         stats = stack.enter_context(tc.tile_pool(name="stats", bufs=6))
         psum = stack.enter_context(tc.psum_pool(name="psum", bufs=1))
 
+        warm_in = const.tile([P, 1], F32)
+        warm_out = const.tile([P, 1], F32)
+        nc.vector.memset(warm_in[:], 0.0)
+        nc.scalar.activation(out=warm_out[:], in_=warm_in[:], func=ACT.Exp)
         ident_f32 = const.tile([P, P], F32)
         make_identity(nc, ident_f32[:])
         ident_bf = const.tile([P, P], BF16)
@@ -147,6 +151,36 @@ def tile_encoderlayer_pa_kernel(tc, q, k, v, out):
             for i in range(4):
                 nc.tensor.transpose(turned[:, i, :], words[:, i * P : (i + 1) * P], order[:])
             copy_out(on_scalar, dest, turned[:])
+
+        def load_first_tiles():
+            first_tiles = []
+            for rows, t, tag, bufs, kept in (
+                (q_rows, 0, "q_half", 6, q_sb), (k_rows, 0, "k_half", 8, k_sb), (k_rows, 1, "k_half", 8, k_sb),
+            ):
+                half_tile = loads.tile([P, ROW // 2], BF16, tag=tag, bufs=bufs, name="half_tile")
+                kept[(t, 0)] = half_tile
+                first_tiles.append((rows, t, half_tile))
+            for pair in range(2):
+                cols = slice(pair * PAIR * FEAT, (pair + 1) * PAIR * FEAT)
+                for rows, t, half_tile in first_tiles:
+                    nc.sync.dma_start(out=half_tile[:, cols], in_=rows[t * P : (t + 1) * P, cols])
+
+        def transpose_two_heads(half_tile, pair, order, dest, on_scalar):
+            words = half_tile[:].bitcast(F32)
+            turned = psum.tile([P, PAIR, P], F32, tag="turned", bufs=3)
+            for i in range(PAIR):
+                head = PAIR * pair + i
+                nc.tensor.transpose(turned[:, i, :], words[:, head * P : (head + 1) * P], order[:])
+            copy_out(on_scalar, dest, turned[:])
+
+        def transpose_first_tiles():
+            qT_tile = work.tile([P, HEADS, P * 2], BF16, tag="qT_tile", bufs=2)
+            qT[0] = qT_tile
+            for pair in range(2):
+                heads = slice(PAIR * pair, PAIR * pair + PAIR)
+                transpose_two_heads(q_sb[(0, 0)], pair, ident_f32, qT_tile[:].bitcast(F32)[:, heads, :], True)
+                transpose_two_heads(k_sb[(0, 0)], pair, key_order, kT_words[:, heads, 0:P], False)
+                transpose_two_heads(k_sb[(1, 0)], pair, key_order, kT_words[:, heads, P : 2 * P], pair == 0)
 
         def transpose_q(t, half, on_scalar):
             if half == 0:
@@ -355,11 +389,12 @@ def tile_encoderlayer_pa_kernel(tc, q, k, v, out):
                     load_v(4, pair)
 
         stack.enter_context(tc.manual_schedule())
-        for half in range(2):
-            load_q(0, half)
-            for t in range(2):
-                load_k(t, half)
-            load_v(0, half)
+        load_first_tiles()
+        load_v(0, 0)
+        load_q(0, 1)
+        for t in range(2):
+            load_k(t, 1)
+        load_v(0, 1)
         load_v(0, 2)
         load_v(0, 3)
         for half in range(2):
@@ -370,9 +405,7 @@ def tile_encoderlayer_pa_kernel(tc, q, k, v, out):
             load_k(3, half)
         for pair in range(STEPS_PER_TILE):
             load_v(2, pair)
-        transpose_q(0, 0, True)
-        for t in range(2):
-            transpose_k(t, 0, t % 2 == 1)
+        transpose_first_tiles()
         for chunk in range(V_AHEAD):
             regroup_v(chunk)
 

import math
from contextlib import ExitStack

import concourse.mybir as mybir
from concourse.masks import make_identity

F32 = mybir.dt.float32
BF16 = mybir.dt.bfloat16
U32 = mybir.dt.uint32
U8 = mybir.dt.uint8
I32 = mybir.dt.int32
FP8X4 = mybir.dt.float8_e4m3fn_x4
ALU = mybir.AluOpType
ACT = mybir.ActivationFunctionType
AXIS = mybir.AxisListType

P = 128
SEQ = 1536
HEADS = 8
FEAT = 256
ROW = HEADS * FEAT
TILES = SEQ // P
PACK = 4
K_PASS = P * PACK
SPAN = 3 * P
PAIR = 2
STEPS_PER_TILE = HEADS // PAIR
STEPS = TILES * STEPS_PER_TILE
GROUPS = 5
OWN_WINDOWS = 3
CHUNKS = OWN_WINDOWS * HEADS
V_AHEAD = 4
SCALE = 1.0 / 16.0
MASKED = -1.0e9 / SCALE

FLOPS = 2 * 2 * HEADS * (SEQ // 256) * 256 * 512 * FEAT


def clamp(x, low, high):
    return max(low, min(x, high))


def tile_encoderlayer_pa_kernel(tc, q, k, v, out):
    nc = tc.nc
    q_rows = q.rearrange("b s h f -> (b s) (h f)")
    k_rows = k.rearrange("b s h f -> (b s) (h f)")
    v_rows = v.rearrange("b s h f -> (b s) (h f)")
    out_rows = out.rearrange("b s h f -> (b s) (h f)")

    with ExitStack() as stack:
        const = stack.enter_context(tc.tile_pool(name="const", bufs=1))
        loads = stack.enter_context(tc.tile_pool(name="loads", bufs=2))
        work = stack.enter_context(tc.tile_pool(name="work", bufs=3))
        stats = stack.enter_context(tc.tile_pool(name="stats", bufs=6))
        psum = stack.enter_context(tc.psum_pool(name="psum", bufs=1))

        warm_in = const.tile([P, 1], F32)
        warm_out = const.tile([P, 1], F32)
        nc.vector.memset(warm_in[:], 0.0)
        nc.scalar.activation(out=warm_out[:], in_=warm_in[:], func=ACT.Exp)
        ident_f32 = const.tile([P, P], F32)
        make_identity(nc, ident_f32[:])
        ident_bf = const.tile([P, P], BF16)
        make_identity(nc, ident_bf[:])

        mask_f32 = const.tile([P, 2, P], F32)
        nc.gpsimd.memset(mask_f32[:], 0.0)
        nc.gpsimd.affine_select(
            out=mask_f32[:, 0, :], in_=mask_f32[:, 0, :], compare_op=ALU.is_ge, fill=MASKED,
            base=0, pattern=[[1, P]], channel_multiplier=-1,
        )
        nc.gpsimd.affine_select(
            out=mask_f32[:, 1, :], in_=mask_f32[:, 1, :], compare_op=ALU.is_ge, fill=MASKED,
            base=0, pattern=[[-1, P]], channel_multiplier=1,
        )
        key_order = const.tile([P, P], F32)
        nc.vector.tensor_copy(
            out=key_order[:].rearrange("i (u c e) -> i u c e", u=2, e=2),
            in_=ident_f32[:].rearrange("i (c u e) -> i u c e", u=2, e=2),
        )
        mask_bf = const.tile([P, 2, P], BF16)
        for block in range(2):
            nc.vector.tensor_copy(
                out=mask_bf[:, block, :].rearrange("q (u c e) -> q u c e", u=2, e=2),
                in_=mask_f32[:, block, :].rearrange("q (c u e) -> q u c e", u=2, e=2),
            )

        e_low = const.tile([P, HEADS, K_PASS], BF16)
        e_high = const.tile([P, HEADS, K_PASS], BF16)
        e_last = const.tile([P, HEADS, K_PASS], BF16)
        e_tiles = [e_low, e_high, e_last]
        nc.vector.memset(e_low[:].rearrange("q h (u c) -> q (h u) c", u=2)[:, :, 128:256], 0.0)
        nc.vector.memset(e_high[:].rearrange("q h (u c) -> q (h u) c", u=2)[:, :, 0:64], 0.0)
        nc.gpsimd.memset(e_last[:].rearrange("q h (u c) -> q (h u) c", u=2)[:, :, 0:128], 0.0)

        kT = const.tile([P, HEADS, SEQ * 2], BF16)
        kT_words = kT[:].bitcast(F32)
        kT_feat = kT[:].rearrange("p h (s e) -> p h s e", e=2)

        v_codes = {}
        v_scales = {}
        for g in range(GROUPS):
            codes = const.tile([P, ROW], U32, name="codes%d" % g, align_bytes=64)
            scales = const.tile([P, ROW], U8, name="scales%d" % g, align_bytes=64)
            v_codes[g] = codes
            v_scales[g] = scales
            if g % 2 == 0:
                nc.vector.memset(scales[:].bitcast(I32), 0)

        q_sb = {}
        k_sb = {}
        v_raw = {}
        qT = {}
        in_flight = {}
        tile_sums = {}
        tile_inverse = {}
        v_grouped_tiles = {}

        def load_rows(rows, t, half, tag, bufs):
            half_tile = loads.tile([P, ROW // 2], BF16, tag=tag, bufs=bufs, name="half_tile")
            cols = slice(half * (ROW // 2), (half + 1) * (ROW // 2))
            nc.sync.dma_start(out=half_tile[:], in_=rows[t * P : (t + 1) * P, cols])
            return half_tile

        def load_q(t, half):
            q_sb[(t, half)] = load_rows(q_rows, t, half, "q_half", 6)

        def load_k(t, half):
            k_sb[(t, half)] = load_rows(k_rows, t, half, "k_half", 8)

        def load_v(g, pair):
            if pair == 0:
                v_tile = loads.tile([P, PACK, ROW], BF16, tag="v_tile", bufs=2)
                v_raw[g] = v_tile
            first = 2 * g * P
            cols = slice(pair * PAIR * FEAT, (pair + 1) * PAIR * FEAT)
            nc.sync.dma_start(
                out=v_raw[g][:, :, cols],
                in_=v_rows[first : first + K_PASS, cols].rearrange("(p j) w -> p j w", j=PACK),
            )

        def copy_out(on_scalar, dest, source):
            if on_scalar:
                nc.scalar.copy(out=dest, in_=source)
            else:
                nc.vector.tensor_copy(out=dest, in_=source)

        def transpose_four_heads(half_tile, order, dest, on_scalar):
            words = half_tile[:].bitcast(F32)
            turned = psum.tile([P, 4, P], F32, tag="turned", bufs=3)
            for i in range(4):
                nc.tensor.transpose(turned[:, i, :], words[:, i * P : (i + 1) * P], order[:])
            copy_out(on_scalar, dest, turned[:])

        def load_first_tiles():
            first_tiles = []
            for rows, t, tag, bufs, kept in (
                (q_rows, 0, "q_half", 6, q_sb), (k_rows, 0, "k_half", 8, k_sb), (k_rows, 1, "k_half", 8, k_sb),
            ):
                half_tile = loads.tile([P, ROW // 2], BF16, tag=tag, bufs=bufs, name="half_tile")
                kept[(t, 0)] = half_tile
                first_tiles.append((rows, t, half_tile))
            for pair in range(2):
                cols = slice(pair * PAIR * FEAT, (pair + 1) * PAIR * FEAT)
                for rows, t, half_tile in first_tiles:
                    nc.sync.dma_start(out=half_tile[:, cols], in_=rows[t * P : (t + 1) * P, cols])

        def transpose_two_heads(half_tile, pair, order, dest, on_scalar):
            words = half_tile[:].bitcast(F32)
            turned = psum.tile([P, PAIR, P], F32, tag="turned", bufs=3)
            for i in range(PAIR):
                head = PAIR * pair + i
                nc.tensor.transpose(turned[:, i, :], words[:, head * P : (head + 1) * P], order[:])
            copy_out(on_scalar, dest, turned[:])

        def transpose_first_tiles():
            qT_tile = work.tile([P, HEADS, P * 2], BF16, tag="qT_tile", bufs=2)
            qT[0] = qT_tile
            for pair in range(2):
                heads = slice(PAIR * pair, PAIR * pair + PAIR)
                transpose_two_heads(q_sb[(0, 0)], pair, ident_f32, qT_tile[:].bitcast(F32)[:, heads, :], True)
                transpose_two_heads(k_sb[(0, 0)], pair, key_order, kT_words[:, heads, 0:P], False)
                transpose_two_heads(k_sb[(1, 0)], pair, key_order, kT_words[:, heads, P : 2 * P], pair == 0)

        def transpose_q(t, half, on_scalar):
            if half == 0:
                qT_tile = work.tile([P, HEADS, P * 2], BF16, tag="qT_tile", bufs=2)
                qT[t] = qT_tile
            dest = qT[t][:].bitcast(F32)[:, 4 * half : 4 * half + 4, :]
            transpose_four_heads(q_sb[(t, half)], ident_f32, dest, on_scalar)

        def transpose_k(t, half, on_scalar):
            dest = kT_words[:, 4 * half : 4 * half + 4, t * P : (t + 1) * P]
            transpose_four_heads(k_sb[(t, half)], key_order, dest, on_scalar)

        def regroup_v(chunk):
            g, h = 2 * (chunk // HEADS), chunk % HEADS
            v_grouped = work.tile([P, FEAT, PACK], BF16, tag="v_grouped", bufs=V_AHEAD, align_bytes=64)
            nc.gpsimd.tensor_scalar(
                out=v_grouped[:],
                in0=v_raw[g][:, :, h * FEAT : (h + 1) * FEAT].rearrange("p j w -> p w j"),
                scalar1=1.0, scalar2=0.0, op0=ALU.mult, op1=ALU.add,
            )
            v_grouped_tiles[chunk] = v_grouped

        def quantise_v(chunk):
            g, h = 2 * (chunk // HEADS), chunk % HEADS
            cols = slice(h * FEAT, (h + 1) * FEAT)
            nc.vector.quantize_mx(
                out=v_codes[g][:, cols].bitcast(FP8X4),
                scales=v_scales[g][:, cols],
                in_=v_grouped_tiles[chunk][:].rearrange("p w j -> p (w j)"),
            )

        def copy_window(g, half):
            cols = slice(half * (ROW // 2), (half + 1) * (ROW // 2))
            for tiles in (v_codes, v_scales):
                nc.sync.dma_start(
                    out=tiles[g][0 : P // 2, cols].bitcast(I32), in_=tiles[g - 1][P // 2 : P, cols].bitcast(I32),
                )
                nc.sync.dma_start(
                    out=tiles[g][P // 2 : P, cols].bitcast(I32), in_=tiles[g + 1][0 : P // 2, cols].bitcast(I32),
                )

        def begin(step):
            t = step // STEPS_PER_TILE
            first_key_tile = max(t - 1, 0)
            key_tiles = min(t + 1, TILES - 1) - first_key_tile + 1
            window = clamp((t - 1) // 2, 0, GROUPS - 1)
            peak = stats.tile([P, PAIR], F32, tag="peak")
            if step % STEPS_PER_TILE == 0:
                row_sums = stats.tile([P, HEADS], F32, tag="row_sums")
                tile_sums[t] = row_sums
            in_flight[step] = {
                "t": t, "first_head": PAIR * (step % STEPS_PER_TILE),
                "first_key_tile": first_key_tile, "window": window,
                "key_tiles": key_tiles,
                "quarter": first_key_tile - 2 * window,
                "peak": peak, "banks": [],
            }

        def scores(step, i):
            state = in_flight[step]
            t = state["t"]
            h = state["first_head"] + i
            if t == 0:
                masked_tiles, blocks = slice(1, 2), slice(1, 2)
            elif t == TILES - 1:
                masked_tiles, blocks = slice(0, 1), slice(0, 1)
            else:
                masked_tiles, blocks = slice(0, 3, 2), slice(0, 2)
            span = state["key_tiles"] * P
            keys = slice(state["first_key_tile"] * P, state["first_key_tile"] * P + span)
            qT_feat = qT[t][:].rearrange("p h (r e) -> p h r e", e=2)
            s_ps = psum.tile([P, SPAN], F32, tag="s_ps", bufs=3)
            for e in range(2):
                nc.tensor.matmul(
                    out=s_ps[:, 0:span], lhsT=qT_feat[:, h, :, e], rhs=kT_feat[:, h, keys, e],
                    start=(e == 0), stop=False,
                )
            nc.tensor.matmul(
                out=s_ps[:].rearrange("q (b c) -> q b c", c=P)[:, masked_tiles, :],
                lhsT=ident_bf[:], rhs=mask_bf[:, blocks, :],
                start=False, stop=True,
            )
            minus_s = work.tile([P, SPAN], F32, tag="minus_s", bufs=6)
            nc.vector.tensor_scalar(
                out=minus_s[:, 0:span], in0=s_ps[:, 0:span], scalar1=-SCALE, scalar2=None, op0=ALU.mult, op1=ALU.min,
                accum_out=state["peak"][:, i : i + 1],
            )
            state["banks"].append(minus_s)

        def shifts(step):
            state = in_flight[step]
            moved = stats.tile([P, PAIR], F32, tag="moved")
            nc.gpsimd.tensor_scalar(
                out=moved[:], in0=state["peak"][:], scalar1=1.0, scalar2=math.log(2.0),
                op0=ALU.mult, op1=ALU.add,
            )
            state["moved"] = moved

        def exponentials(step):
            state = in_flight[step]
            quarter = state["quarter"]
            key_tiles = state["key_tiles"]
            moved = state["moved"]
            for i in range(PAIR):
                h = state["first_head"] + i
                e_view = e_tiles[quarter][:, h, :].rearrange("q (u b x) -> q b u x", u=2, b=4)
                nc.scalar.activation(
                    out=e_view[:, quarter : quarter + key_tiles, :, :],
                    in_=state["banks"][i][:, 0 : key_tiles * P].rearrange("q (b u x) -> q b u x", b=key_tiles, u=2),
                    func=ACT.Exp, bias=moved[:, i : i + 1], scale=-1.0,
                    accum_out=tile_sums[state["t"]][:, h : h + 1],
                )

        def transpose_e(step):
            state = in_flight[step]
            e_words = e_tiles[state["quarter"]][:].bitcast(F32)
            turned = psum.tile([P, PAIR, 2, P], F32, tag="turned", bufs=3)
            for i in range(PAIR):
                h = state["first_head"] + i
                for u in range(2):
                    nc.tensor.transpose(turned[:, i, u, :], e_words[:, h, u * P : (u + 1) * P], ident_f32[:])
            e_grouped = work.tile([P, PAIR * P * PACK], BF16, tag="e_grouped", align_bytes=64)
            copy_out(
                True,
                e_grouped[:].bitcast(F32).rearrange("p (i q u) -> p i q u", i=PAIR, u=2),
                turned[:].rearrange("p i u q -> p i q u"),
            )
            state["e_grouped"] = e_grouped

        def quantise_e(step):
            state = in_flight[step]
            e_codes = work.tile([P, PAIR * P], U32, tag="e_codes", align_bytes=64)
            e_scales = work.tile([P, PAIR * P], U8, tag="e_scales", align_bytes=64)
            nc.vector.quantize_mx(
                out=e_codes[:].bitcast(FP8X4), scales=e_scales[:], in_=state["e_grouped"][:],
            )
            state["e_codes"] = e_codes
            state["e_scales"] = e_scales

        def invert_row_sums(t):
            inverse = stats.tile([P, HEADS], F32, tag="inverse")
            nc.vector.reciprocal(out=inverse[:], in_=tile_sums[t][:])
            tile_inverse[t] = inverse

        def weighted_sums(step):
            state = in_flight[step]
            g = state["window"]
            o_ps = psum.tile([P, PAIR, FEAT], F32, tag="o_ps", bufs=2)
            for i in range(PAIR):
                h = state["first_head"] + i
                queries = slice(i * P, (i + 1) * P)
                cols = slice(h * FEAT, (h + 1) * FEAT)
                nc.tensor.matmul_mx(
                    out=o_ps[:, i, :],
                    lhsT=state["e_codes"][:, queries].bitcast(FP8X4),
                    lhsT_scale=state["e_scales"][:, queries],
                    rhs=v_codes[g][:, cols].bitcast(FP8X4),
                    rhs_scale=v_scales[g][:, cols],
                    start=True, stop=True,
                )
            state["o_ps"] = o_ps

        def divide_and_store(step):
            state = in_flight[step]
            t = state["t"]
            first_head = state["first_head"]
            o_sb = work.tile([P, PAIR, FEAT], F32, tag="o_sb", bufs=4)
            nc.vector.tensor_tensor(
                out=o_sb[:], in0=state["o_ps"][:],
                in1=tile_inverse[t][:, first_head : first_head + PAIR].unsqueeze(2).to_broadcast([P, PAIR, FEAT]),
                op=ALU.mult,
            )
            nc.sync.dma_start(
                out=out_rows[t * P : (t + 1) * P, first_head * FEAT : (first_head + PAIR) * FEAT],
                in_=o_sb[:].rearrange("q i f -> q (i f)"),
            )

        def transposes_ahead(step):
            t = step // STEPS_PER_TILE
            part = step % STEPS_PER_TILE
            if step == 0:
                transpose_q(0, 1, True)
                transpose_k(0, 1, True)
            elif step == 1:
                transpose_k(1, 1, True)
                transpose_k(2, 0, True)
            elif step == 2:
                transpose_q(1, 0, True)
                transpose_k(2, 1, True)
            elif step == 3:
                transpose_q(1, 1, True)
            elif part % 2 == 0 and t + 1 < TILES:
                transpose_q(t + 1, part // 2, True)
            elif part % 2 == 1 and t + 2 < TILES:
                transpose_k(t + 2, part // 2, True)

        def loads_ahead(t):
            for half in range(2):
                if t + 2 < TILES:
                    load_q(t + 2, half)
            for half in range(2):
                if t + 4 < TILES:
                    load_k(t + 4, half)
            for pair in range(STEPS_PER_TILE):
                if t == 2:
                    load_v(4, pair)

        stack.enter_context(tc.manual_schedule())
        load_first_tiles()
        load_v(0, 0)
        load_q(0, 1)
        for t in range(2):
            load_k(t, 1)
        load_v(0, 1)
        load_v(0, 2)
        load_v(0, 3)
        for half in range(2):
            load_k(2, half)
        for half in range(2):
            load_q(1, half)
        for half in range(2):
            load_k(3, half)
        for pair in range(STEPS_PER_TILE):
            load_v(2, pair)
        transpose_first_tiles()
        for chunk in range(V_AHEAD):
            regroup_v(chunk)

        def live(step):
            return 0 <= step < STEPS

        def chunk_round(chunk):
            if chunk < 2 * HEADS:
                return chunk
            return 2 * chunk - 15

        next_chunk = 0
        for rnd in range(STEPS + 6):
            if live(rnd):
                if rnd % STEPS_PER_TILE == 0:
                    loads_ahead(rnd // STEPS_PER_TILE)
                begin(rnd)
                scores(rnd, 0)
            if live(rnd - 5):
                weighted_sums(rnd - 5)
                divide_and_store(rnd - 5)
            if live(rnd):
                scores(rnd, 1)
                shifts(rnd)
            if live(rnd - 1):
                exponentials(rnd - 1)
            if live(rnd - 2):
                transpose_e(rnd - 2)
            if live(rnd):
                transposes_ahead(rnd)
            first_chunk = next_chunk
            while next_chunk < CHUNKS and chunk_round(next_chunk) <= rnd:
                quantise_v(next_chunk)
                if next_chunk >= HEADS and next_chunk % 4 == 3:
                    copy_window(2 * (next_chunk // HEADS) - 1, (next_chunk % HEADS) // 4)
                next_chunk += 1
            for chunk in range(first_chunk + V_AHEAD, min(next_chunk + V_AHEAD, CHUNKS)):
                regroup_v(chunk)
            if live(rnd - 3):
                quantise_e(rnd - 3)
            if live(rnd - 1) and rnd % STEPS_PER_TILE == 0:
                invert_row_sums((rnd - 1) // STEPS_PER_TILE)
